import numpy as np
import ml_dtypes


def mxq(x, axis, fmt="e4m3"):
    dtype, down = {"e4m3": (ml_dtypes.float8_e4m3fn, 7), "e5m2": (ml_dtypes.float8_e5m2, 14)}[fmt]
    v = np.moveaxis(np.asarray(x, np.float32).astype(ml_dtypes.bfloat16).astype(np.float64), axis, -1)
    blocks = v.reshape(v.shape[:-1] + (-1, 32))
    amax = np.abs(blocks).max(-1, keepdims=True)
    byte = np.maximum(np.where(amax > 0, np.frexp(amax)[1] - 1 + 127, 0) - down, 1)
    scale = np.exp2(byte - 127.0)
    codes = (blocks / scale).astype(np.float32).astype(dtype).astype(np.float64)
    return np.moveaxis((codes * scale).reshape(v.shape), -1, axis)


WIDE = False


def mx_kscale(k):
    if not WIDE:
        return np.ones(k)
    levels = np.array([10, -10, 5, -5, 0])
    a = np.random.permutation(np.resize(levels, k // 512 * 4)).reshape(k // 512, 4)
    idx = np.arange(k)
    return np.exp2(a[idx // 512, idx % 128 // 32])


BF16 = ml_dtypes.bfloat16


def bf(x):
    return np.asarray(x, np.float32).astype(BF16)


def f64(x):
    return np.asarray(x).astype(np.float64)


E2M1 = np.array([0.0, 0.5, 1.0, 1.5, 2.0, 3.0, 4.0, 6.0, -0.0, -0.5, -1.0, -1.5, -2.0, -3.0, -4.0, -6.0])


def pack_weight(w, fmt):
    k, n = w.shape
    w = f64(bf(w)).reshape(k // 32, 32, n)
    amax = np.abs(w).max(1)
    if fmt == "e4m3":
        byte = np.frexp(amax)[1] - 1 + 127 - 7
    else:
        mant, ex = np.frexp(amax / 6.0)
        byte = np.where(mant > 0.5, ex, ex - 1) + 127
    byte = np.clip(np.where(amax > 0, byte, 1), 1, 254)
    scaled = (w * np.exp2(127.0 - byte)[:, None, :]).reshape(k, n).astype(np.float32)
    by_word = np.ascontiguousarray(scaled.reshape(k // 512, 128, 4, n).transpose(0, 1, 3, 2))
    if fmt == "e4m3":
        words = by_word.astype(ml_dtypes.float8_e4m3fn).view(np.uint8)
    else:
        c = by_word.astype(ml_dtypes.float4_e2m1fn).view(np.uint8) & 0xF
        words = c[..., 0::2] | (c[..., 1::2] << 4)
    return np.ascontiguousarray(words), np.ascontiguousarray(byte.astype(np.uint8).reshape(k // 512, 16, n))


def unpack_weight(words, scales, fmt):
    g, p, n, _ = words.shape
    if fmt == "e4m3":
        vals = np.ascontiguousarray(words).view(ml_dtypes.float8_e4m3fn).astype(np.float64)
    else:
        nib = np.empty((g, p, n, 4), np.uint8)
        nib[..., 0::2] = words & 0xF
        nib[..., 1::2] = words >> 4
        vals = E2M1[nib]
    vals = vals * np.repeat(np.exp2(scales.astype(np.float64) - 127.0), 8, axis=1)[..., None]
    return vals.transpose(0, 1, 3, 2).reshape(g * 512, n)

def pack4(w):
    words, scales = pack_weight(w, "e2m1")
    return words.reshape(words.shape[0], 128, -1), scales


def unpack4(words, scales):
    return unpack_weight(words.reshape(words.shape[0], 128, -1, 2), scales, "e2m1")


N, M, D, B = 256, 512, 4, 1024
MD = M * D


def sigmoid(v):
    return 1.0 / (1.0 + np.exp(-v))


def diag_mask():
    return np.broadcast_to((1.0 - np.eye(M))[:, :, None], (M, M, D)).reshape(M, MD)


def tri_mask():
    return f64(np.arange(D)[:, None] < np.arange(D)[None, :])


def big_diag(w):
    w3 = w.reshape(M, M, D).copy()
    i = np.arange(M)
    w3[i, i, :] = np.random.standard_normal((M, D)) * 0.5
    return w3.reshape(M, MD)


def setup_inputs():
    r = np.random.standard_normal
    s = mx_kscale(M)
    ca, cb = 0.7 / np.sqrt(M), 0.7 / np.sqrt(N)
    x_t = bf(r((B, N)))
    m_t = bf(r((B, M)) * s)
    a_t = bf(r((B, MD)))
    A_fg_words, A_fg_scales = pack4(r((M, MD)) * ca / s[:, None])
    A_in_words, A_in_scales = pack4(r((M, MD)) * ca / s[:, None])
    return {"x_t": x_t, "m_t": m_t, "a_t": a_t,
            "A_fg_words": A_fg_words, "A_fg_scales": A_fg_scales,
            "A_in_words": A_in_words, "A_in_scales": A_in_scales,
            "A_th": bf(big_diag(r((M, MD)) * ca)), "A_pt_blk": bf(r((M, D, D)) * 0.4),
            "B_fg": bf(r((N, MD)) * cb), "B_in": bf(r((N, MD)) * cb), "B_th": bf(r((N, MD)) * cb),
            "b_fg": bf(r((1, MD)) * 0.3), "b_in": bf(r((1, MD)) * 0.3), "b_th": bf(r((1, MD)) * 0.3)}


def reference(x_t, m_t, a_t, A_fg_words, A_fg_scales, A_in_words, A_in_scales, A_th, A_pt_blk, B_fg, B_in, B_th, b_fg, b_in, b_th):
    x, a = f64(x_t), f64(a_t)
    mq = mxq(f64(m_t), 1, "e4m3")
    G_fg = sigmoid((mq @ unpack4(A_fg_words, A_fg_scales)) + x @ f64(B_fg) + f64(b_fg))
    G_in = sigmoid((mq @ unpack4(A_in_words, A_in_scales)) + x @ f64(B_in) + f64(b_in))
    a3 = a.reshape(B, M, D)
    P = f64(A_pt_blk) * tri_mask()
    pt = np.zeros((B, M, D))
    for s in range(D):
        pt = pt + a3[:, :, s, None] * P[None, :, s, :]
    a_last = a3[:, :, -1]
    G_th = np.tanh(pt.reshape(B, MD) + (mxq(a_last, 1, "e4m3") @ mxq(f64(A_th) * diag_mask(), 0, "e4m3"))
                   + x @ f64(B_th) + f64(b_th))
    return a * G_fg + G_th * G_in

@@ -1,0 +1,348 @@
+from contextlib import ExitStack
+
+import concourse.bass as bass
+import concourse.mybir as mybir
+import concourse.tile as tile
+from concourse.masks import make_identity
+
+F32 = mybir.dt.float32
+BF16 = mybir.dt.bfloat16
+U8 = mybir.dt.uint8
+U32 = mybir.dt.uint32
+I32 = mybir.dt.int32
+FP8X4 = mybir.dt.float8_e4m3fn_x4
+FP4X4 = mybir.dt.float4_e2m1fn_x4
+ACT = mybir.ActivationFunctionType
+ALU = mybir.AluOpType
+AX = mybir.AxisListType
+
+P = 128
+ROWS = 1024
+ROW_TILES = ROWS // P
+UNITS = 512
+SLOTS = 4
+COLS = UNITS * SLOTS
+BANK = 512
+BANKS_PER_ROW = COLS // BANK
+PAIR = 2 * BANK
+XDIM = 256
+X_PASSES = XDIM // P
+CHUNKS = COLS // P
+UNITS_PER_CHUNK = P // SLOTS
+
+FLOPS = 2 * ROWS * COLS * (3 * UNITS + 3 * XDIM)
+
+GATES = ("fg", "in", "th")
+
+
+def tile_edrncell_pa_kernel(
+    tc,
+    x_t,
+    m_t,
+    a_t,
+    A_fg_words,
+    A_fg_scales,
+    A_in_words,
+    A_in_scales,
+    A_th,
+    A_pt_blk,
+    B_fg,
+    B_in,
+    B_th,
+    b_fg,
+    b_in,
+    b_th,
+    out,
+):
+    nc = tc.nc
+    with ExitStack() as stack:
+        keep = stack.enter_context(tc.tile_pool(name="keep", bufs=1))
+        stage = stack.enter_context(tc.tile_pool(name="stage", bufs=2))
+        sums = stack.enter_context(tc.tile_pool(name="sums", bufs=4))
+        gates = stack.enter_context(tc.tile_pool(name="gates", bufs=4))
+        acc = stack.enter_context(tc.psum_pool(name="acc", bufs=6))
+        flip = stack.enter_context(tc.psum_pool(name="flip", bufs=2))
+
+        given_words = {"fg": A_fg_words, "in": A_in_words}
+        given_scales = {"fg": A_fg_scales, "in": A_in_scales}
+        planes = {}
+        for gate in ("fg", "in"):
+            planes[gate] = keep.tile([P, COLS], U8, name="plane_%s" % gate, align_bytes=64)
+            nc.vector.memset(planes[gate][:].bitcast(I32), 0)
+        for gate in ("fg", "in"):
+            for b in range(2):
+                for r in range(4):
+                    nc.sync.dma_start(
+                        out=planes[gate][32 * b + r : P : 64, :].bitcast(I32),
+                        in_=given_scales[gate][0, 4 * b + r : 16 : 8, :].bitcast(I32),
+                    )
+
+        warm = keep.tile([P, 1], F32, name="warm")
+        nc.vector.memset(warm[:], 0.0)
+        nc.scalar.activation(out=warm[:], in_=warm[:], func=ACT.Sigmoid)
+
+        m_sb, x_sb, a_sb = [], [], []
+
+        def load_rows(i):
+            rows = slice(i * P, (i + 1) * P)
+            m_sb.append(keep.tile([P, UNITS], BF16, name="m_sb%d" % i))
+            x_sb.append(keep.tile([P, XDIM], BF16, name="x_sb%d" % i))
+            a_sb.append(keep.tile([P, COLS], BF16, name="a_sb%d" % i))
+            nc.sync.dma_start(out=m_sb[i][:], in_=m_t[rows, :])
+            nc.sync.dma_start(out=x_sb[i][:], in_=x_t[rows, :])
+            nc.sync.dma_start(out=a_sb[i][:], in_=a_t[rows, :])
+
+        words = {"fg": [], "in": []}
+        b_sb = {"fg": [], "in": [], "th": []}
+        b_dram = {"fg": B_fg, "in": B_in, "th": B_th}
+        th_raw = []
+
+        def load_columns(h):
+            cols = slice(h * BANK, (h + 1) * BANK)
+            for gate in GATES:
+                if gate == "th":
+                    raw = stage.tile([P, 4, BANK], BF16, name="th_raw", bufs=BANKS_PER_ROW)
+                    nc.sync.dma_start(out=raw[:], in_=A_th.rearrange("(t p) n -> p t n", p=P)[:, :, cols])
+                    th_raw.append(raw)
+                else:
+                    w = keep.tile([P, 2 * BANK], U8, name="words_%s%d" % (gate, h), align_bytes=64)
+                    nc.sync.dma_start(
+                        out=w[:].bitcast(I32),
+                        in_=given_words[gate][0, :, 2 * h * BANK : 2 * (h + 1) * BANK].bitcast(I32),
+                    )
+                    words[gate].append(w)
+                bt = keep.tile([P, X_PASSES, BANK], BF16, name="b_%s%d" % (gate, h))
+                nc.sync.dma_start(out=bt[:], in_=b_dram[gate].rearrange("(k p) n -> p k n", p=P)[:, :, cols])
+                b_sb[gate].append(bt)
+
+        bias = {}
+        for gate, vec in (("fg", b_fg), ("in", b_in)):
+            bias[gate] = keep.tile([P, COLS], BF16, name="bias_%s" % gate)
+            nc.scalar.dma_start(out=bias[gate][:], in_=vec.rearrange("o n -> (o n)").partition_broadcast(P))
+        pt_raw = keep.tile([P, CHUNKS, SLOTS], BF16, name="pt_raw")
+        nc.scalar.dma_start(
+            out=pt_raw[:],
+            in_=A_pt_blk.rearrange("j s t -> (j s) t").rearrange("(c q) t -> q c t", q=P),
+        )
+
+        th_bias_rows = keep.tile([P, CHUNKS, SLOTS], BF16, name="th_bias_rows")
+        nc.vector.memset(th_bias_rows[:], 0.0)
+        nc.scalar.dma_start(
+            out=th_bias_rows[SLOTS - 1 : P : SLOTS, :, :],
+            in_=b_th.rearrange("o (c u t) -> (o u) c t", c=CHUNKS, t=SLOTS),
+        )
+
+        ident_bf = keep.tile([P, P], BF16, name="ident_bf")
+        make_identity(nc, ident_bf[:])
+        ident_f32 = keep.tile([P, P], F32, name="ident_f32")
+        make_identity(nc, ident_f32[:])
+        not_ident = keep.tile([P, P], BF16, name="not_ident")
+        nc.vector.tensor_scalar(
+            out=not_ident[:], in0=ident_bf[:], scalar1=-1.0, scalar2=1.0, op0=ALU.mult, op1=ALU.add
+        )
+
+        th_words, th_planes = [], []
+
+        def quantise_th(h):
+            raw = th_raw[h]
+            own = raw[:, h, :].rearrange("p (q s) -> p q s", s=SLOTS)
+            nc.vector.tensor_tensor(
+                out=own, in0=own, in1=not_ident[:].unsqueeze(2).to_broadcast([P, P, SLOTS]), op=ALU.mult
+            )
+            grouped = stage.tile([P, BANK, 4], BF16, name="th_grouped", align_bytes=64)
+            nc.vector.tensor_copy(out=grouped[:], in_=raw[:].rearrange("p t n -> p n t"))
+            w = keep.tile([P, BANK], U32, name="th_words%d" % h, align_bytes=64)
+            s = keep.tile([P, BANK], U8, name="th_plane%d" % h, align_bytes=64)
+            nc.vector.quantize_mx(
+                out=w[:].bitcast(FP8X4), scales=s[:], in_=grouped[:].rearrange("p n t -> p (n t)")
+            )
+            th_words.append(w)
+            th_planes.append(s)
+
+        slot_is = keep.tile([P, SLOTS], F32, name="slot_is")
+        nc.vector.tensor_reduce(
+            out=slot_is[:], in_=ident_f32[:].rearrange("q (u s) -> q s u", s=SLOTS), axis=AX.X, op=ALU.add
+        )
+        unit_is = keep.tile([P, UNITS_PER_CHUNK], F32, name="unit_is")
+        nc.vector.tensor_reduce(
+            out=unit_is[:], in_=ident_f32[:].rearrange("q (u s) -> q u s", s=SLOTS), axis=AX.X, op=ALU.add
+        )
+        feeds = keep.tile([P, SLOTS], F32, name="feeds")
+        nc.vector.memset(feeds[:, 0:1], 0.0)
+        for t in range(1, SLOTS):
+            nc.vector.tensor_tensor(
+                out=feeds[:, t : t + 1], in0=feeds[:, t - 1 : t], in1=slot_is[:, t - 1 : t], op=ALU.add
+            )
+        pt_rows = keep.tile([P, CHUNKS, SLOTS], BF16, name="pt_rows")
+        nc.vector.tensor_tensor(
+            out=pt_rows[:],
+            in0=pt_raw[:],
+            in1=feeds[:].unsqueeze(1).to_broadcast([P, CHUNKS, SLOTS]),
+            op=ALU.mult,
+        )
+        nc.vector.tensor_tensor(out=pt_rows[:], in0=pt_rows[:], in1=th_bias_rows[:], op=ALU.add)
+        is_last_slot = slot_is[:, SLOTS - 1 : SLOTS]
+        not_last_slot = keep.tile([P, 1], F32, name="not_last_slot")
+        nc.vector.tensor_scalar(
+            out=not_last_slot[:], in0=is_last_slot, scalar1=-1.0, scalar2=1.0, op0=ALU.mult, op1=ALU.add
+        )
+        blk = keep.tile([P, CHUNKS, UNITS_PER_CHUNK, SLOTS], BF16, name="blk")
+        blk_shape = [P, CHUNKS, UNITS_PER_CHUNK, SLOTS]
+        nc.vector.tensor_tensor(
+            out=blk[:],
+            in0=pt_rows[:].unsqueeze(2).to_broadcast(blk_shape),
+            in1=unit_is[:].unsqueeze(1).unsqueeze(3).to_broadcast(blk_shape),
+            op=ALU.mult,
+        )
+
+        mq_words = keep.tile([P, ROW_TILES, P], U32, name="mq_words", align_bytes=64)
+        mq_plane = keep.tile([P, ROW_TILES, P], U8, name="mq_plane", align_bytes=64)
+        aq_words = keep.tile([P, ROW_TILES, P], U32, name="aq_words", align_bytes=64)
+        aq_plane = keep.tile([P, ROW_TILES, P], U8, name="aq_plane", align_bytes=64)
+        xT = keep.tile([P, X_PASSES, ROWS], BF16, name="xT")
+        aT = {}
+
+        def flip_small(i):
+            rows = slice(i * P, (i + 1) * P)
+            m_flip = flip.tile([P, 2, P], F32, name="m_flip", tag="flip")
+            m_pairs = m_sb[i][:].bitcast(F32)
+            for u in range(2):
+                nc.tensor.transpose(m_flip[:, u, :], m_pairs[:, u : UNITS // 2 : 2], ident_f32[:])
+            ax_flip = flip.tile([P, 4 + X_PASSES, P], BF16, name="ax_flip", tag="flip")
+            for t in range(4):
+                nc.tensor.transpose(
+                    ax_flip[:, t, :], a_sb[i][:, BANK * t + 3 : BANK * (t + 1) : SLOTS], ident_bf[:]
+                )
+            for k in range(X_PASSES):
+                nc.tensor.transpose(ax_flip[:, 4 + k, :], x_sb[i][:, k * P : (k + 1) * P], ident_bf[:])
+            m_grouped = stage.tile([P, P, 4], BF16, name="m_grouped", align_bytes=64)
+            nc.scalar.copy(
+                out=m_grouped[:].rearrange("p b t -> p (b t)").bitcast(F32).rearrange("p (b u) -> p b u", u=2),
+                in_=m_flip[:].rearrange("p u b -> p b u"),
+            )
+            l_grouped = stage.tile([P, P, 4], BF16, name="l_grouped", align_bytes=64)
+            nc.scalar.copy(out=l_grouped[:], in_=ax_flip[:, 0:4, :].rearrange("p t b -> p b t"))
+            nc.scalar.copy(out=xT[:, :, rows], in_=ax_flip[:, 4 : 4 + X_PASSES, :])
+            nc.vector.quantize_mx(
+                out=mq_words[:, i, :].bitcast(FP8X4),
+                scales=mq_plane[:, i, :],
+                in_=m_grouped[:].rearrange("p b t -> p (b t)"),
+            )
+            nc.vector.quantize_mx(
+                out=aq_words[:, i, :].bitcast(FP8X4),
+                scales=aq_plane[:, i, :],
+                in_=l_grouped[:].rearrange("p b t -> p (b t)"),
+            )
+
+        def flip_a(i):
+            aT[i] = stage.tile([P, CHUNKS, P], BF16, name="aT")
+            for half in range(2):
+                a_flip = flip.tile([P, CHUNKS // 2, P], BF16, name="a_flip", tag="flip")
+                for c in range(CHUNKS // 2):
+                    chunk = half * (CHUNKS // 2) + c
+                    nc.tensor.transpose(a_flip[:, c, :], a_sb[i][:, chunk * P : (chunk + 1) * P], ident_bf[:])
+                nc.scalar.activation(
+                    out=aT[i][:, half * (CHUNKS // 2) : (half + 1) * (CHUNKS // 2), :],
+                    in_=a_flip[:],
+                    func=ACT.Identity,
+                    scale=not_last_slot[:],
+                    bias=is_last_slot,
+                )
+
+        func = {"fg": ACT.Sigmoid, "in": ACT.Sigmoid, "th": ACT.Tanh}
+
+        def gate_tile(gate, i, h, dest):
+            rows = slice(i * P, (i + 1) * P)
+            cols = slice(h * BANK, (h + 1) * BANK)
+            plain = acc.tile([P, BANK], F32, name="plain", tag="acc")
+            for k in range(X_PASSES):
+                nc.tensor.matmul(
+                    plain[:],
+                    lhsT=xT[:, k, rows],
+                    rhs=b_sb[gate][h][:, k, :],
+                    start=(k == 0),
+                    stop=(k == X_PASSES - 1 and gate != "th"),
+                )
+            if gate == "th":
+                per_bank = BANK // P
+                for q in range(per_bank):
+                    chunk = h * per_bank + q
+                    nc.tensor.matmul(
+                        plain[:, q * P : (q + 1) * P],
+                        lhsT=aT[i][:, chunk, :],
+                        rhs=blk[:, chunk, :, :].rearrange("q u t -> q (u t)"),
+                        start=False,
+                        stop=(q == per_bank - 1),
+                    )
+            mx = acc.tile([P, BANK], F32, name="mx", tag="acc")
+            if gate == "th":
+                nc.tensor.matmul_mx(
+                    out=mx[:],
+                    lhsT=aq_words[:, i, :].bitcast(FP8X4),
+                    lhsT_scale=aq_plane[:, i, :],
+                    rhs=th_words[h][:].bitcast(FP8X4),
+                    rhs_scale=th_planes[h][:],
+                    start=True,
+                    stop=True,
+                )
+            else:
+                nc.tensor.matmul_mx(
+                    out=mx[:],
+                    lhsT=mq_words[:, i, :].bitcast(FP8X4),
+                    lhsT_scale=mq_plane[:, i, :],
+                    rhs=words[gate][h][:].bitcast(FP4X4),
+                    rhs_scale=planes[gate][:, cols],
+                    start=True,
+                    stop=True,
+                )
+            partial = sums.tile([P, BANK], F32, name="partial")
+            if gate == "th":
+                nc.scalar.copy(out=partial[:], in_=plain[:])
+            else:
+                nc.vector.tensor_tensor(out=partial[:], in0=plain[:], in1=bias[gate][:, cols], op=ALU.add)
+            nc.vector.tensor_tensor(out=dest, in0=mx[:], in1=partial[:], op=ALU.add)
+            nc.scalar.activation(out=dest, in_=dest, func=func[gate])
+
+        def combine(engine, g, a_part):
+            engine.tensor_tensor(out=g["fg"], in0=g["fg"], in1=a_part, op=ALU.mult)
+            engine.tensor_tensor(out=g["th"], in0=g["th"], in1=g["in"], op=ALU.mult)
+            engine.tensor_tensor(out=g["fg"], in0=g["fg"], in1=g["th"], op=ALU.add)
+
+        load_rows(0)
+        load_columns(0)
+        load_columns(1)
+        load_rows(1)
+        load_columns(2)
+        load_columns(3)
+        for i in range(2, ROW_TILES):
+            load_rows(i)
+
+        flip_small(0)
+        flip_a(0)
+        for h in range(BANKS_PER_ROW):
+            quantise_th(h)
+
+        for i in range(ROW_TILES):
+            rows = slice(i * P, (i + 1) * P)
+            last = i == ROW_TILES - 1
+            for pair in range(COLS // PAIR):
+                g = {}
+                for gate in GATES:
+                    g[gate] = gates.tile([P, PAIR], F32, name="g_%s" % gate)
+                for hh in range(PAIR // BANK):
+                    h = pair * (PAIR // BANK) + hh
+                    part = slice(hh * BANK, (hh + 1) * BANK)
+                    cols = slice(h * BANK, (h + 1) * BANK)
+                    for gate in GATES:
+                        gate_tile(gate, i, h, g[gate][:, part])
+                    if last:
+                        combine(nc.vector, {gate: g[gate][:, part] for gate in GATES}, a_sb[i][:, cols])
+                        nc.sync.dma_start(out=out[rows, cols], in_=g["fg"][:, part])
+                if not last:
+                    cols = slice(pair * PAIR, (pair + 1) * PAIR)
+                    combine(nc.gpsimd, {gate: g[gate][:] for gate in GATES}, a_sb[i][:, cols])
+                    nc.sync.dma_start(out=out[rows, cols], in_=g["fg"][:])
+                    if pair == 0:
+                        flip_small(i + 1)
+                    else:
+                        flip_a(i + 1)

@@ -23,12 +23,13 @@ UNITS = 512
 SLOTS = 4
 COLS = UNITS * SLOTS
 BANK = 512
-BANKS_PER_ROW = COLS // BANK
-PAIR = 2 * BANK
+BLOCKS = COLS // BANK
 XDIM = 256
 X_PASSES = XDIM // P
 CHUNKS = COLS // P
-UNITS_PER_CHUNK = P // SLOTS
+PER_BANK = BANK // P
+UPC = P // SLOTS
+PAIRS = ROW_TILES // 2
 
 FLOPS = 2 * ROWS * COLS * (3 * UNITS + 3 * XDIM)
 
@@ -58,97 +59,187 @@ def tile_edrncell_pa_kernel(
     with ExitStack() as stack:
         keep = stack.enter_context(tc.tile_pool(name="keep", bufs=1))
         stage = stack.enter_context(tc.tile_pool(name="stage", bufs=2))
-        sums = stack.enter_context(tc.tile_pool(name="sums", bufs=4))
-        gates = stack.enter_context(tc.tile_pool(name="gates", bufs=4))
+        sums = stack.enter_context(tc.tile_pool(name="sums", bufs=6))
+        gates = stack.enter_context(tc.tile_pool(name="gates", bufs=3))
         acc = stack.enter_context(tc.psum_pool(name="acc", bufs=6))
         flip = stack.enter_context(tc.psum_pool(name="flip", bufs=2))
+        stack.enter_context(tc.manual_schedule())
+
+        x_rows = x_t.rearrange("(p i) c -> p i c", i=ROW_TILES)
+        m_rows = m_t.rearrange("(p i) c -> p i c", i=ROW_TILES)
+        a_rows = a_t.rearrange("(p i) c -> p i c", i=ROW_TILES)
+        out_rows = out.rearrange("(p i) c -> p i c", i=ROW_TILES)
+
+        bias_rows = keep.tile([P, P], BF16, name="bias_rows")
+        nc.vector.memset(bias_rows[:].bitcast(I32), 0)
+        pt_in = keep.tile([P, UPC, SLOTS, SLOTS], BF16, name="pt_in")
+        nc.vector.memset(pt_in[:], 0.0)
+        th_bias_in = keep.tile([P, UPC, SLOTS], BF16, name="th_bias_in")
+        nc.vector.memset(th_bias_in[:], 0.0)
+        warm = keep.tile([P, 1], F32, name="warm")
+        nc.vector.memset(warm[:], 0.0)
+        nc.scalar.dma_start(out=pt_in[0:CHUNKS, :, :, :], in_=A_pt_blk.rearrange("(c u) s t -> c u s t", c=CHUNKS))
+        nc.scalar.dma_start(out=bias_rows[0:CHUNKS, :], in_=b_fg.rearrange("o (c n) -> (o c) n", c=CHUNKS))
+        nc.scalar.dma_start(out=bias_rows[CHUNKS : 2 * CHUNKS, :], in_=b_in.rearrange("o (c n) -> (o c) n", c=CHUNKS))
+        nc.scalar.dma_start(
+            out=th_bias_in[0:CHUNKS, :, :], in_=b_th.rearrange("o (c u t) -> (o c) u t", c=CHUNKS, t=SLOTS)
+        )
+        nc.scalar.activation(out=warm[:], in_=warm[:], func=ACT.Sigmoid)
+
+        ident_f32 = keep.tile([P, P], F32, name="ident_f32")
+        make_identity(nc, ident_f32[:])
+        ident_bf = keep.tile([P, P], BF16, name="ident_bf")
+        nc.vector.tensor_copy(out=ident_bf[:], in_=ident_f32[:])
 
         given_words = {"fg": A_fg_words, "in": A_in_words}
         given_scales = {"fg": A_fg_scales, "in": A_in_scales}
+        b_dram = {"fg": B_fg, "in": B_in, "th": B_th}
         planes = {}
         for gate in ("fg", "in"):
             planes[gate] = keep.tile([P, COLS], U8, name="plane_%s" % gate, align_bytes=64)
             nc.vector.memset(planes[gate][:].bitcast(I32), 0)
-        for gate in ("fg", "in"):
-            for b in range(2):
+        words = {}
+        b_sb = {}
+        th_raw = {}
+        m_sb = {}
+        a_sb = {}
+
+        def load_b(gate, h):
+            t = keep.tile([P, X_PASSES, BANK], BF16, name="b_%s%d" % (gate, h))
+            nc.sync.dma_start(
+                out=t[:], in_=b_dram[gate].rearrange("(k p) n -> p k n", p=P)[:, :, h * BANK : (h + 1) * BANK]
+            )
+            b_sb[gate, h] = t
+
+        def load_words(gate, h):
+            w = keep.tile([P, 2 * BANK], U8, name="words_%s%d" % (gate, h), align_bytes=64)
+            nc.sync.dma_start(
+                out=w[:].bitcast(I32),
+                in_=given_words[gate][0, :, 2 * h * BANK : 2 * (h + 1) * BANK].bitcast(I32),
+            )
+            words[gate, h] = w
+
+        def load_scales():
+            for gate in ("fg", "in"):
                 for r in range(4):
                     nc.sync.dma_start(
-                        out=planes[gate][32 * b + r : P : 64, :].bitcast(I32),
-                        in_=given_scales[gate][0, 4 * b + r : 16 : 8, :].bitcast(I32),
+                        out=planes[gate][r : P : 32, :].bitcast(I32),
+                        in_=given_scales[gate][0, r : 16 : 4, :].bitcast(I32),
                     )
 
-        warm = keep.tile([P, 1], F32, name="warm")
-        nc.vector.memset(warm[:], 0.0)
-        nc.scalar.activation(out=warm[:], in_=warm[:], func=ACT.Sigmoid)
+        def load_th(h):
+            raw = stage.tile([P, 4, BANK], BF16, name="th_raw", bufs=BLOCKS)
+            nc.sync.dma_start(
+                out=raw[:], in_=A_th.rearrange("(t p) n -> p t n", p=P)[:, :, h * BANK : (h + 1) * BANK]
+            )
+            th_raw[h] = raw
 
-        m_sb, x_sb, a_sb = [], [], []
+        def load_m(j):
+            m_sb[j] = keep.tile([P, 2, UNITS], BF16, name="m_sb%d" % j)
+            nc.sync.dma_start(out=m_sb[j][:], in_=m_rows[:, 2 * j : 2 * j + 2, :])
 
-        def load_rows(i):
-            rows = slice(i * P, (i + 1) * P)
-            m_sb.append(keep.tile([P, UNITS], BF16, name="m_sb%d" % i))
-            x_sb.append(keep.tile([P, XDIM], BF16, name="x_sb%d" % i))
-            a_sb.append(keep.tile([P, COLS], BF16, name="a_sb%d" % i))
-            nc.sync.dma_start(out=m_sb[i][:], in_=m_t[rows, :])
-            nc.sync.dma_start(out=x_sb[i][:], in_=x_t[rows, :])
-            nc.sync.dma_start(out=a_sb[i][:], in_=a_t[rows, :])
+        def load_a(j):
+            a_sb[j] = keep.tile([P, 2, COLS], BF16, name="a_sb%d" % j)
+            for i in range(2):
+                nc.sync.dma_start(out=a_sb[j][:, i, :], in_=a_rows[:, 2 * j + i, :])
 
-        words = {"fg": [], "in": []}
-        b_sb = {"fg": [], "in": [], "th": []}
-        b_dram = {"fg": B_fg, "in": B_in, "th": B_th}
-        th_raw = []
+        x_sb = keep.tile([P, ROW_TILES, XDIM], BF16, name="x_sb")
+        nc.sync.dma_start(out=x_sb[:, 0:2, :], in_=x_rows[:, 0:2, :])
+        load_b("fg", 0)
+        load_m(0)
+        load_words("fg", 0)
+        load_scales()
+        load_b("in", 0)
+        load_words("in", 0)
+        load_th(0)
+        load_a(0)
+        load_b("th", 0)
+        for h in range(1, BLOCKS):
+            load_th(h)
+            load_b("fg", h)
+            load_words("fg", h)
+            load_b("in", h)
+            load_words("in", h)
+            load_b("th", h)
+            if h == 1:
+                nc.sync.dma_start(out=x_sb[:, 2:ROW_TILES, :], in_=x_rows[:, 2:ROW_TILES, :])
+                load_m(1)
+            if h == 2:
+                load_a(1)
+        for j in range(2, PAIRS):
+            load_m(j)
+            load_a(j)
 
-        def load_columns(h):
-            cols = slice(h * BANK, (h + 1) * BANK)
-            for gate in GATES:
-                if gate == "th":
-                    raw = stage.tile([P, 4, BANK], BF16, name="th_raw", bufs=BANKS_PER_ROW)
-                    nc.sync.dma_start(out=raw[:], in_=A_th.rearrange("(t p) n -> p t n", p=P)[:, :, cols])
-                    th_raw.append(raw)
-                else:
-                    w = keep.tile([P, 2 * BANK], U8, name="words_%s%d" % (gate, h), align_bytes=64)
-                    nc.sync.dma_start(
-                        out=w[:].bitcast(I32),
-                        in_=given_words[gate][0, :, 2 * h * BANK : 2 * (h + 1) * BANK].bitcast(I32),
-                    )
-                    words[gate].append(w)
-                bt = keep.tile([P, X_PASSES, BANK], BF16, name="b_%s%d" % (gate, h))
-                nc.sync.dma_start(out=bt[:], in_=b_dram[gate].rearrange("(k p) n -> p k n", p=P)[:, :, cols])
-                b_sb[gate].append(bt)
-
-        bias = {}
-        for gate, vec in (("fg", b_fg), ("in", b_in)):
-            bias[gate] = keep.tile([P, COLS], BF16, name="bias_%s" % gate)
-            nc.scalar.dma_start(out=bias[gate][:], in_=vec.rearrange("o n -> (o n)").partition_broadcast(P))
-        pt_raw = keep.tile([P, CHUNKS, SLOTS], BF16, name="pt_raw")
-        nc.scalar.dma_start(
-            out=pt_raw[:],
-            in_=A_pt_blk.rearrange("j s t -> (j s) t").rearrange("(c q) t -> q c t", q=P),
-        )
-
-        th_bias_rows = keep.tile([P, CHUNKS, SLOTS], BF16, name="th_bias_rows")
-        nc.vector.memset(th_bias_rows[:], 0.0)
-        nc.scalar.dma_start(
-            out=th_bias_rows[SLOTS - 1 : P : SLOTS, :, :],
-            in_=b_th.rearrange("o (c u t) -> (o u) c t", c=CHUNKS, t=SLOTS),
-        )
-
-        ident_bf = keep.tile([P, P], BF16, name="ident_bf")
-        make_identity(nc, ident_bf[:])
-        ident_f32 = keep.tile([P, P], F32, name="ident_f32")
-        make_identity(nc, ident_f32[:])
         not_ident = keep.tile([P, P], BF16, name="not_ident")
         nc.vector.tensor_scalar(
             out=not_ident[:], in0=ident_bf[:], scalar1=-1.0, scalar2=1.0, op0=ALU.mult, op1=ALU.add
         )
+        unit_is = keep.tile([P, UPC], F32, name="unit_is")
+        nc.vector.tensor_reduce(
+            out=unit_is[:], in_=ident_f32[:].rearrange("q (u s) -> q u s", s=SLOTS), axis=AX.X, op=ALU.add
+        )
+        is_last = keep.tile([P, 1], F32, name="is_last")
+        nc.vector.tensor_reduce(out=is_last[:], in_=ident_f32[:, SLOTS - 1 : P : SLOTS], axis=AX.X, op=ALU.add)
+        not_last = keep.tile([P, 1], F32, name="not_last")
+        nc.vector.tensor_scalar(
+            out=not_last[:], in0=is_last[:], scalar1=-1.0, scalar2=1.0, op0=ALU.mult, op1=ALU.add
+        )
+        for s in range(SLOTS - 1):
+            nc.vector.memset(pt_in[:, :, s, 0 : s + 1], 0.0)
+        nc.vector.tensor_copy(out=pt_in[:, :, SLOTS - 1, :], in_=th_bias_in[:])
 
-        th_words, th_planes = [], []
+        pt_rows = keep.tile([P, CHUNKS, SLOTS], BF16, name="pt_rows")
+        blk = keep.tile([P, CHUNKS, UPC, SLOTS], BF16, name="blk")
+
+        def turn_pt():
+            pt_flip = flip.tile([P, SLOTS, P], BF16, name="pt_flip", tag="flip")
+            pt_cols = pt_in[:].rearrange("p u s t -> p (u s t)")
+            for t in range(SLOTS):
+                nc.tensor.transpose(pt_flip[:, t, :], pt_cols[:, t : BANK : SLOTS], ident_bf[:])
+            nc.vector.tensor_copy(out=pt_rows[:], in_=pt_flip[:, :, 0:CHUNKS].rearrange("q t c -> q c t"))
+
+        def build_blk(h):
+            shape = [P, PER_BANK, UPC, SLOTS]
+            part = slice(h * PER_BANK, (h + 1) * PER_BANK)
+            nc.gpsimd.tensor_tensor(
+                out=blk[:, part, :, :],
+                in0=pt_rows[:, part, :].unsqueeze(2).to_broadcast(shape),
+                in1=unit_is[:].unsqueeze(1).unsqueeze(3).to_broadcast(shape),
+                op=ALU.mult,
+            )
+
+        bias = {}
+        bias_cols = keep.tile([P, 2 * CHUNKS], BF16, name="bias_cols")
+
+        def turn_bias():
+            bias_flip = flip.tile([P, P], BF16, name="bias_flip", tag="flip")
+            nc.tensor.transpose(bias_flip[:], bias_rows[:], ident_bf[:])
+            nc.vector.tensor_copy(out=bias_cols[:], in_=bias_flip[:, 0 : 2 * CHUNKS])
+
+        def spread_bias(h):
+            spread = flip.tile([P, 2, PER_BANK, P], BF16, name="spread", tag="flip")
+            both = keep.tile([P, 2, BANK], BF16, name="bias%d" % h)
+            for k in range(2):
+                for q in range(PER_BANK):
+                    col = k * CHUNKS + h * PER_BANK + q
+                    nc.tensor.transpose(
+                        spread[:, k, q, :], bias_cols[:, col : col + 1].to_broadcast([P, P]), ident_bf[:]
+                    )
+            nc.scalar.copy(out=both[:], in_=spread[:].rearrange("p k q n -> p k (q n)"))
+            bias["fg", h] = both[:, 0, :]
+            bias["in", h] = both[:, 1, :]
+
+        th_words, th_planes = {}, {}
+
+        def mask_th(h):
+            raw = th_raw[h]
+            own = raw[:, h, :].rearrange("p (q s) -> p q s", s=SLOTS)
+            (nc.gpsimd if h == 0 else nc.vector).tensor_tensor(
+                out=own, in0=own, in1=not_ident[:].unsqueeze(2).to_broadcast([P, P, SLOTS]), op=ALU.mult
+            )
 
         def quantise_th(h):
             raw = th_raw[h]
-            own = raw[:, h, :].rearrange("p (q s) -> p q s", s=SLOTS)
-            nc.vector.tensor_tensor(
-                out=own, in0=own, in1=not_ident[:].unsqueeze(2).to_broadcast([P, P, SLOTS]), op=ALU.mult
-            )
             grouped = stage.tile([P, BANK, 4], BF16, name="th_grouped", align_bytes=64)
             nc.vector.tensor_copy(out=grouped[:], in_=raw[:].rearrange("p t n -> p n t"))
             w = keep.tile([P, BANK], U32, name="th_words%d" % h, align_bytes=64)
@@ -156,193 +247,209 @@ def tile_edrncell_pa_kernel(
             nc.vector.quantize_mx(
                 out=w[:].bitcast(FP8X4), scales=s[:], in_=grouped[:].rearrange("p n t -> p (n t)")
             )
-            th_words.append(w)
-            th_planes.append(s)
+            th_words[h] = w
+            th_planes[h] = s
 
-        slot_is = keep.tile([P, SLOTS], F32, name="slot_is")
-        nc.vector.tensor_reduce(
-            out=slot_is[:], in_=ident_f32[:].rearrange("q (u s) -> q s u", s=SLOTS), axis=AX.X, op=ALU.add
-        )
-        unit_is = keep.tile([P, UNITS_PER_CHUNK], F32, name="unit_is")
-        nc.vector.tensor_reduce(
-            out=unit_is[:], in_=ident_f32[:].rearrange("q (u s) -> q u s", s=SLOTS), axis=AX.X, op=ALU.add
-        )
-        feeds = keep.tile([P, SLOTS], F32, name="feeds")
-        nc.vector.memset(feeds[:, 0:1], 0.0)
-        for t in range(1, SLOTS):
-            nc.vector.tensor_tensor(
-                out=feeds[:, t : t + 1], in0=feeds[:, t - 1 : t], in1=slot_is[:, t - 1 : t], op=ALU.add
-            )
-        pt_rows = keep.tile([P, CHUNKS, SLOTS], BF16, name="pt_rows")
-        nc.vector.tensor_tensor(
-            out=pt_rows[:],
-            in0=pt_raw[:],
-            in1=feeds[:].unsqueeze(1).to_broadcast([P, CHUNKS, SLOTS]),
-            op=ALU.mult,
-        )
-        nc.vector.tensor_tensor(out=pt_rows[:], in0=pt_rows[:], in1=th_bias_rows[:], op=ALU.add)
-        is_last_slot = slot_is[:, SLOTS - 1 : SLOTS]
-        not_last_slot = keep.tile([P, 1], F32, name="not_last_slot")
-        nc.vector.tensor_scalar(
-            out=not_last_slot[:], in0=is_last_slot, scalar1=-1.0, scalar2=1.0, op0=ALU.mult, op1=ALU.add
-        )
-        blk = keep.tile([P, CHUNKS, UNITS_PER_CHUNK, SLOTS], BF16, name="blk")
-        blk_shape = [P, CHUNKS, UNITS_PER_CHUNK, SLOTS]
-        nc.vector.tensor_tensor(
-            out=blk[:],
-            in0=pt_rows[:].unsqueeze(2).to_broadcast(blk_shape),
-            in1=unit_is[:].unsqueeze(1).unsqueeze(3).to_broadcast(blk_shape),
-            op=ALU.mult,
-        )
+        xT, mq, aq, aT = {}, {}, {}, {}
+        late = []
 
-        mq_words = keep.tile([P, ROW_TILES, P], U32, name="mq_words", align_bytes=64)
-        mq_plane = keep.tile([P, ROW_TILES, P], U8, name="mq_plane", align_bytes=64)
-        aq_words = keep.tile([P, ROW_TILES, P], U32, name="aq_words", align_bytes=64)
-        aq_plane = keep.tile([P, ROW_TILES, P], U8, name="aq_plane", align_bytes=64)
-        xT = keep.tile([P, X_PASSES, ROWS], BF16, name="xT")
-        aT = {}
+        def run_late():
+            while late:
+                late.pop(0)()
 
-        def flip_small(i):
-            rows = slice(i * P, (i + 1) * P)
-            m_flip = flip.tile([P, 2, P], F32, name="m_flip", tag="flip")
-            m_pairs = m_sb[i][:].bitcast(F32)
-            for u in range(2):
-                nc.tensor.transpose(m_flip[:, u, :], m_pairs[:, u : UNITS // 2 : 2], ident_f32[:])
-            ax_flip = flip.tile([P, 4 + X_PASSES, P], BF16, name="ax_flip", tag="flip")
-            for t in range(4):
-                nc.tensor.transpose(
-                    ax_flip[:, t, :], a_sb[i][:, BANK * t + 3 : BANK * (t + 1) : SLOTS], ident_bf[:]
-                )
-            for k in range(X_PASSES):
-                nc.tensor.transpose(ax_flip[:, 4 + k, :], x_sb[i][:, k * P : (k + 1) * P], ident_bf[:])
-            m_grouped = stage.tile([P, P, 4], BF16, name="m_grouped", align_bytes=64)
-            nc.scalar.copy(
-                out=m_grouped[:].rearrange("p b t -> p (b t)").bitcast(F32).rearrange("p (b u) -> p b u", u=2),
-                in_=m_flip[:].rearrange("p u b -> p b u"),
-            )
-            l_grouped = stage.tile([P, P, 4], BF16, name="l_grouped", align_bytes=64)
-            nc.scalar.copy(out=l_grouped[:], in_=ax_flip[:, 0:4, :].rearrange("p t b -> p b t"))
-            nc.scalar.copy(out=xT[:, :, rows], in_=ax_flip[:, 4 : 4 + X_PASSES, :])
+        def flip_x(j):
+            x_flip = flip.tile([P, 2, X_PASSES, P], BF16, name="x_flip", tag="flip")
+            for i in range(2):
+                for k in range(X_PASSES):
+                    nc.tensor.transpose(x_flip[:, i, k, :], x_sb[:, 2 * j + i, k * P : (k + 1) * P], ident_bf[:])
+            xT[j] = keep.tile([P, 2, X_PASSES, P], BF16, name="xT%d" % j)
+            nc.scalar.copy(out=xT[j][:], in_=x_flip[:])
+
+        def quantise_rows(name, grouped, j):
+            w = keep.tile([P, 2, P], U32, name="%s_words%d" % (name, j), align_bytes=64)
+            s = keep.tile([P, 2, P], U8, name="%s_plane%d" % (name, j), align_bytes=64)
             nc.vector.quantize_mx(
-                out=mq_words[:, i, :].bitcast(FP8X4),
-                scales=mq_plane[:, i, :],
-                in_=m_grouped[:].rearrange("p b t -> p (b t)"),
+                out=w[:].rearrange("p i b -> p (i b)").bitcast(FP8X4),
+                scales=s[:].rearrange("p i b -> p (i b)"),
+                in_=grouped[:].rearrange("p i b t -> p (i b t)"),
             )
-            nc.vector.quantize_mx(
-                out=aq_words[:, i, :].bitcast(FP8X4),
-                scales=aq_plane[:, i, :],
-                in_=l_grouped[:].rearrange("p b t -> p (b t)"),
-            )
+            return w, s
 
-        def flip_a(i):
-            aT[i] = stage.tile([P, CHUNKS, P], BF16, name="aT")
-            for half in range(2):
-                a_flip = flip.tile([P, CHUNKS // 2, P], BF16, name="a_flip", tag="flip")
-                for c in range(CHUNKS // 2):
-                    chunk = half * (CHUNKS // 2) + c
-                    nc.tensor.transpose(a_flip[:, c, :], a_sb[i][:, chunk * P : (chunk + 1) * P], ident_bf[:])
-                nc.scalar.activation(
-                    out=aT[i][:, half * (CHUNKS // 2) : (half + 1) * (CHUNKS // 2), :],
-                    in_=a_flip[:],
-                    func=ACT.Identity,
-                    scale=not_last_slot[:],
-                    bias=is_last_slot,
-                )
+        def flip_m(j):
+            m_flip = flip.tile([P, 2, 2, P], F32, name="m_flip", tag="flip")
+            for i in range(2):
+                m_pairs = m_sb[j][:, i, :].bitcast(F32)
+                for u in range(2):
+                    nc.tensor.transpose(m_flip[:, i, u, :], m_pairs[:, u : UNITS // 2 : 2], ident_f32[:])
+            grouped = stage.tile([P, 2, P, 4], BF16, name="m_grouped", align_bytes=64)
+            (nc.vector.tensor_copy if j == 0 else nc.scalar.copy)(
+                out=grouped[:].rearrange("p i b t -> p (i b t)").bitcast(F32).rearrange("p (i b u) -> p i b u", i=2, u=2),
+                in_=m_flip[:].rearrange("p i u b -> p i b u"),
+            )
+            late.append(lambda: mq.update({j: quantise_rows("mq", grouped, j)}))
+
+        def flip_last(j):
+            l_flip = flip.tile([P, 2, 4, P], BF16, name="l_flip", tag="flip")
+            for i in range(2):
+                for t in range(4):
+                    nc.tensor.transpose(
+                        l_flip[:, i, t, :], a_sb[j][:, i, BANK * t + 3 : BANK * (t + 1) : SLOTS], ident_bf[:]
+                    )
+            grouped = stage.tile([P, 2, P, 4], BF16, name="l_grouped", align_bytes=64)
+            nc.scalar.copy(out=grouped[:], in_=l_flip[:].rearrange("p i t b -> p i b t"))
+            late.append(lambda: aq.update({j: quantise_rows("aq", grouped, j)}))
+
+        def flip_a(j, i, half):
+            if half == 0:
+                aT[j, i] = stage.tile([P, CHUNKS, P], BF16, name="aT", bufs=4)
+            part = slice(half * (CHUNKS // 2), (half + 1) * (CHUNKS // 2))
+            a_flip = flip.tile([P, CHUNKS // 2, P], BF16, name="a_flip", tag="flip")
+            for c in range(CHUNKS // 2):
+                chunk = half * (CHUNKS // 2) + c
+                nc.tensor.transpose(a_flip[:, c, :], a_sb[j][:, i, chunk * P : (chunk + 1) * P], ident_bf[:])
+            nc.scalar.activation(
+                out=aT[j, i][:, part, :], in_=a_flip[:], func=ACT.Identity, scale=not_last[:], bias=is_last[:]
+            )
 
         func = {"fg": ACT.Sigmoid, "in": ACT.Sigmoid, "th": ACT.Tanh}
+        partial = {}
+        g = {}
 
-        def gate_tile(gate, i, h, dest):
-            rows = slice(i * P, (i + 1) * P)
-            cols = slice(h * BANK, (h + 1) * BANK)
-            plain = acc.tile([P, BANK], F32, name="plain", tag="acc")
+        def plain(gate, j, i, h):
+            bank = acc.tile([P, BANK], F32, name="plain", tag="acc")
             for k in range(X_PASSES):
                 nc.tensor.matmul(
-                    plain[:],
-                    lhsT=xT[:, k, rows],
-                    rhs=b_sb[gate][h][:, k, :],
+                    bank[:],
+                    lhsT=xT[j][:, i, k, :],
+                    rhs=b_sb[gate, h][:, k, :],
                     start=(k == 0),
                     stop=(k == X_PASSES - 1 and gate != "th"),
                 )
             if gate == "th":
-                per_bank = BANK // P
-                for q in range(per_bank):
-                    chunk = h * per_bank + q
+                for q in range(PER_BANK):
+                    chunk = h * PER_BANK + q
                     nc.tensor.matmul(
-                        plain[:, q * P : (q + 1) * P],
-                        lhsT=aT[i][:, chunk, :],
+                        bank[:, q * P : (q + 1) * P],
+                        lhsT=aT[j, i][:, chunk, :],
                         rhs=blk[:, chunk, :, :].rearrange("q u t -> q (u t)"),
                         start=False,
-                        stop=(q == per_bank - 1),
+                        stop=(q == PER_BANK - 1),
                     )
-            mx = acc.tile([P, BANK], F32, name="mx", tag="acc")
+            part = sums.tile([P, BANK], F32, name="partial")
             if gate == "th":
-                nc.tensor.matmul_mx(
-                    out=mx[:],
-                    lhsT=aq_words[:, i, :].bitcast(FP8X4),
-                    lhsT_scale=aq_plane[:, i, :],
-                    rhs=th_words[h][:].bitcast(FP8X4),
-                    rhs_scale=th_planes[h][:],
-                    start=True,
-                    stop=True,
-                )
+                nc.scalar.copy(out=part[:], in_=bank[:])
             else:
-                nc.tensor.matmul_mx(
-                    out=mx[:],
-                    lhsT=mq_words[:, i, :].bitcast(FP8X4),
-                    lhsT_scale=mq_plane[:, i, :],
-                    rhs=words[gate][h][:].bitcast(FP4X4),
-                    rhs_scale=planes[gate][:, cols],
-                    start=True,
-                    stop=True,
-                )
-            partial = sums.tile([P, BANK], F32, name="partial")
+                nc.vector.tensor_tensor(out=part[:], in0=bank[:], in1=bias[gate, h], op=ALU.add)
+            partial[gate, i] = part
+
+        def mx(gate, j, i, h):
+            bank = acc.tile([P, BANK], F32, name="mx", tag="acc")
+            w, s = aq[j] if gate == "th" else mq[j]
             if gate == "th":
-                nc.scalar.copy(out=partial[:], in_=plain[:])
+                rhs, rhs_scale = th_words[h][:].bitcast(FP8X4), th_planes[h][:]
             else:
-                nc.vector.tensor_tensor(out=partial[:], in0=plain[:], in1=bias[gate][:, cols], op=ALU.add)
-            nc.vector.tensor_tensor(out=dest, in0=mx[:], in1=partial[:], op=ALU.add)
+                rhs = words[gate, h][:].bitcast(FP4X4)
+                rhs_scale = planes[gate][:, h * BANK : (h + 1) * BANK]
+            nc.tensor.matmul_mx(
+                out=bank[:],
+                lhsT=w[:, i, :].bitcast(FP8X4),
+                lhsT_scale=s[:, i, :],
+                rhs=rhs,
+                rhs_scale=rhs_scale,
+                start=True,
+                stop=True,
+            )
+            if (gate, h) not in g:
+                g[gate, h] = gates.tile([P, 2, BANK], F32, name="g_%s" % gate)
+            dest = g[gate, h][:, i, :]
+            nc.vector.tensor_tensor(out=dest, in0=bank[:], in1=partial[gate, i][:], op=ALU.add)
             nc.scalar.activation(out=dest, in_=dest, func=func[gate])
 
-        def combine(engine, g, a_part):
-            engine.tensor_tensor(out=g["fg"], in0=g["fg"], in1=a_part, op=ALU.mult)
-            engine.tensor_tensor(out=g["th"], in0=g["th"], in1=g["in"], op=ALU.mult)
-            engine.tensor_tensor(out=g["fg"], in0=g["fg"], in1=g["th"], op=ALU.add)
+        def combine(engine, j, h, tiles):
+            cols = slice(h * BANK, (h + 1) * BANK)
+            f, n, t = (g[gate, h][:, tiles, :] for gate in GATES)
+            engine.tensor_tensor(out=f, in0=f, in1=a_sb[j][:, tiles, cols], op=ALU.mult)
+            engine.tensor_tensor(out=t, in0=t, in1=n, op=ALU.mult)
+            engine.tensor_tensor(out=f, in0=f, in1=t, op=ALU.add)
+            nc.sync.dma_start(out=out_rows[:, 2 * j + tiles.start : 2 * j + tiles.stop, cols], in_=f)
 
-        load_rows(0)
-        load_columns(0)
-        load_columns(1)
-        load_rows(1)
-        load_columns(2)
-        load_columns(3)
-        for i in range(2, ROW_TILES):
-            load_rows(i)
+        turn_pt()
+        build_blk(0)
+        turn_bias()
+        flip_x(0)
+        spread_bias(0)
+        flip_m(0)
+        run_late()
+        mask_th(0)
+        for h in range(1, BLOCKS):
+            build_blk(h)
 
-        flip_small(0)
-        flip_a(0)
-        for h in range(BANKS_PER_ROW):
-            quantise_th(h)
-
-        for i in range(ROW_TILES):
-            rows = slice(i * P, (i + 1) * P)
-            last = i == ROW_TILES - 1
-            for pair in range(COLS // PAIR):
-                g = {}
+        def finish(j, h):
+            if j == PAIRS - 1 and h >= BLOCKS - 1:
+                tail.append((j, h))
+            else:
+                combine(nc.gpsimd, j, h, slice(0, 2))
                 for gate in GATES:
-                    g[gate] = gates.tile([P, PAIR], F32, name="g_%s" % gate)
-                for hh in range(PAIR // BANK):
-                    h = pair * (PAIR // BANK) + hh
-                    part = slice(hh * BANK, (hh + 1) * BANK)
-                    cols = slice(h * BANK, (h + 1) * BANK)
+                    g.pop((gate, h))
+
+        tail = []
+
+        for j in range(PAIRS):
+            flips = {}
+            if j + 1 < PAIRS:
+                flips = {
+                    1: lambda: flip_x(j + 1),
+                    2: lambda: flip_m(j + 1),
+                    4: lambda: flip_last(j + 1),
+                    5: lambda: flip_a(j + 1, 0, 0),
+                    6: lambda: flip_a(j + 1, 1, 0),
+                    7: lambda: flip_a(j + 1, 0, 1),
+                }
+            for h in range(BLOCKS):
+                if j == 0 and h == 0:
+                    for i in range(2):
+                        for gate in ("fg", "in"):
+                            plain(gate, j, i, h)
+                            if i == 1 and gate == "fg":
+                                flip_last(0)
+                                flip_a(0, 0, 0)
+                            if i == 1 and gate == "in":
+                                run_late()
+                        for gate in ("fg", "in"):
+                            mx(gate, j, i, h)
+                        if i == 0:
+                            quantise_th(0)
+                    flip_a(0, 1, 0)
+                    mask_th(1)
+                    spread_bias(1)
+                    for i in range(2):
+                        plain("th", j, i, h)
+                    quantise_th(1)
+                    flip_x(1)
+                    flip_a(0, 0, 1)
+                    for i in range(2):
+                        mx("th", j, i, h)
+                    flip_a(0, 1, 1)
+                    finish(j, h)
+                    continue
+                for i in range(2):
+                    step = 2 * h + i
+                    plain("fg", j, i, h)
+                    if step in flips:
+                        flips[step]()
+                    if step == 0 and j > 0:
+                        flip_a(j, 1, 1)
+                    plain("in", j, i, h)
+                    plain("th", j, i, h)
                     for gate in GATES:
-                        gate_tile(gate, i, h, g[gate][:, part])
-                    if last:
-                        combine(nc.vector, {gate: g[gate][:, part] for gate in GATES}, a_sb[i][:, cols])
-                        nc.sync.dma_start(out=out[rows, cols], in_=g["fg"][:, part])
-                if not last:
-                    cols = slice(pair * PAIR, (pair + 1) * PAIR)
-                    combine(nc.gpsimd, {gate: g[gate][:] for gate in GATES}, a_sb[i][:, cols])
-                    nc.sync.dma_start(out=out[rows, cols], in_=g["fg"][:])
-                    if pair == 0:
-                        flip_small(i + 1)
-                    else:
-                        flip_a(i + 1)
+                        mx(gate, j, i, h)
+                        if gate == "in" and step not in flips:
+                            run_late()
+                    if i == 0 and j == 0 and h + 1 < BLOCKS:
+                        mask_th(h + 1)
+                        spread_bias(h + 1)
+                        quantise_th(h + 1)
+                finish(j, h)
+        for j, h in tail:
+            for i in range(2):
+                combine(nc.vector, j, h, slice(i, i + 1))

@@ -59,11 +59,12 @@ def tile_edrncell_pa_kernel(
     with ExitStack() as stack:
         keep = stack.enter_context(tc.tile_pool(name="keep", bufs=1))
         stage = stack.enter_context(tc.tile_pool(name="stage", bufs=2))
-        sums = stack.enter_context(tc.tile_pool(name="sums", bufs=6))
+        sums = stack.enter_context(tc.tile_pool(name="sums", bufs=3))
         gates = stack.enter_context(tc.tile_pool(name="gates", bufs=3))
+        outs = stack.enter_context(tc.tile_pool(name="outs", bufs=3))
         acc = stack.enter_context(tc.psum_pool(name="acc", bufs=6))
         flip = stack.enter_context(tc.psum_pool(name="flip", bufs=2))
-        stack.enter_context(tc.manual_schedule())
+        stack.enter_context(tc.manual_schedule(engines={mybir.EngineType.PE}))
 
         x_rows = x_t.rearrange("(p i) c -> p i c", i=ROW_TILES)
         m_rows = m_t.rearrange("(p i) c -> p i c", i=ROW_TILES)
@@ -226,8 +227,7 @@ def tile_edrncell_pa_kernel(
                         spread[:, k, q, :], bias_cols[:, col : col + 1].to_broadcast([P, P]), ident_bf[:]
                     )
             nc.scalar.copy(out=both[:], in_=spread[:].rearrange("p k q n -> p k (q n)"))
-            bias["fg", h] = both[:, 0, :]
-            bias["in", h] = both[:, 1, :]
+            bias[h] = both
 
         th_words, th_planes = {}, {}
 
@@ -253,9 +253,11 @@ def tile_edrncell_pa_kernel(
         xT, mq, aq, aT = {}, {}, {}, {}
         late = []
 
+        clock = [0]
+
         def run_late():
-            while late:
-                late.pop(0)()
+            while late and late[0][0] < clock[0]:
+                late.pop(0)[1]()
 
         def flip_x(j):
             x_flip = flip.tile([P, 2, X_PASSES, P], BF16, name="x_flip", tag="flip")
@@ -286,7 +288,7 @@ def tile_edrncell_pa_kernel(
                 out=grouped[:].rearrange("p i b t -> p (i b t)").bitcast(F32).rearrange("p (i b u) -> p i b u", i=2, u=2),
                 in_=m_flip[:].rearrange("p i u b -> p i b u"),
             )
-            late.append(lambda: mq.update({j: quantise_rows("mq", grouped, j)}))
+            late.append((clock[0], lambda: mq.update({j: quantise_rows("mq", grouped, j)})))
 
         def flip_last(j):
             l_flip = flip.tile([P, 2, 4, P], BF16, name="l_flip", tag="flip")
@@ -297,7 +299,7 @@ def tile_edrncell_pa_kernel(
                     )
             grouped = stage.tile([P, 2, P, 4], BF16, name="l_grouped", align_bytes=64)
             nc.scalar.copy(out=grouped[:], in_=l_flip[:].rearrange("p i t b -> p i b t"))
-            late.append(lambda: aq.update({j: quantise_rows("aq", grouped, j)}))
+            late.append((clock[0], lambda: aq.update({j: quantise_rows("aq", grouped, j)})))
 
         def flip_a(j, i, half):
             if half == 0:
@@ -311,39 +313,19 @@ def tile_edrncell_pa_kernel(
                 out=aT[j, i][:, part, :], in_=a_flip[:], func=ACT.Identity, scale=not_last[:], bias=is_last[:]
             )
 
-        func = {"fg": ACT.Sigmoid, "in": ACT.Sigmoid, "th": ACT.Tanh}
-        partial = {}
-        g = {}
+        pre, g = {}, {}
 
-        def plain(gate, j, i, h):
-            bank = acc.tile([P, BANK], F32, name="plain", tag="acc")
+        def x_passes(bank, gate, j, i, h):
             for k in range(X_PASSES):
                 nc.tensor.matmul(
-                    bank[:],
+                    bank,
                     lhsT=xT[j][:, i, k, :],
                     rhs=b_sb[gate, h][:, k, :],
                     start=(k == 0),
                     stop=(k == X_PASSES - 1 and gate != "th"),
                 )
-            if gate == "th":
-                for q in range(PER_BANK):
-                    chunk = h * PER_BANK + q
-                    nc.tensor.matmul(
-                        bank[:, q * P : (q + 1) * P],
-                        lhsT=aT[j, i][:, chunk, :],
-                        rhs=blk[:, chunk, :, :].rearrange("q u t -> q (u t)"),
-                        start=False,
-                        stop=(q == PER_BANK - 1),
-                    )
-            part = sums.tile([P, BANK], F32, name="partial")
-            if gate == "th":
-                nc.scalar.copy(out=part[:], in_=bank[:])
-            else:
-                nc.vector.tensor_tensor(out=part[:], in0=bank[:], in1=bias[gate, h], op=ALU.add)
-            partial[gate, i] = part
 
-        def mx(gate, j, i, h):
-            bank = acc.tile([P, BANK], F32, name="mx", tag="acc")
+        def mx_pass(bank, gate, j, i, h):
             w, s = aq[j] if gate == "th" else mq[j]
             if gate == "th":
                 rhs, rhs_scale = th_words[h][:].bitcast(FP8X4), th_planes[h][:]
@@ -351,7 +333,7 @@ def tile_edrncell_pa_kernel(
                 rhs = words[gate, h][:].bitcast(FP4X4)
                 rhs_scale = planes[gate][:, h * BANK : (h + 1) * BANK]
             nc.tensor.matmul_mx(
-                out=bank[:],
+                out=bank,
                 lhsT=w[:, i, :].bitcast(FP8X4),
                 lhsT_scale=s[:, i, :],
                 rhs=rhs,
@@ -359,19 +341,61 @@ def tile_edrncell_pa_kernel(
                 start=True,
                 stop=True,
             )
-            if (gate, h) not in g:
-                g[gate, h] = gates.tile([P, 2, BANK], F32, name="g_%s" % gate)
-            dest = g[gate, h][:, i, :]
-            nc.vector.tensor_tensor(out=dest, in0=bank[:], in1=partial[gate, i][:], op=ALU.add)
-            nc.scalar.activation(out=dest, in_=dest, func=func[gate])
 
-        def combine(engine, j, h, tiles):
+        def plain_two(j, i, h, between=None):
+            pre[i] = sums.tile([P, 3, BANK], F32, name="pre")
+            for k, gate in enumerate(("fg", "in")):
+                bank = acc.tile([P, BANK], F32, name="plain", tag="acc")
+                x_passes(bank[:], gate, j, i, h)
+                nc.vector.tensor_tensor(out=pre[i][:, k, :], in0=bank[:], in1=bias[h][:, k, :], op=ALU.add)
+                if k == 0 and between is not None:
+                    between()
+
+        def plain_th(j, i, h):
+            bank = acc.tile([P, BANK], F32, name="plain", tag="acc")
+            x_passes(bank[:], "th", j, i, h)
+            for q in range(PER_BANK):
+                chunk = h * PER_BANK + q
+                nc.tensor.matmul(
+                    bank[:, q * P : (q + 1) * P],
+                    lhsT=aT[j, i][:, chunk, :],
+                    rhs=blk[:, chunk, :, :].rearrange("q u t -> q (u t)"),
+                    start=False,
+                    stop=(q == PER_BANK - 1),
+                )
+            nc.scalar.copy(out=pre[i][:, 2, :], in_=bank[:])
+
+        def mx_two(j, i, h):
+            for k, gate in enumerate(("fg", "in")):
+                bank = acc.tile([P, BANK], F32, name="mx", tag="acc")
+                mx_pass(bank[:], gate, j, i, h)
+                nc.vector.tensor_tensor(out=pre[i][:, k, :], in0=bank[:], in1=pre[i][:, k, :], op=ALU.add)
+            if i == 0:
+                g["fi"] = gates.tile([P, 2, 2, BANK], F32, name="g_fi")
+            nc.scalar.activation(out=g["fi"][:, :, i, :], in_=pre[i][:, 0:2, :], func=ACT.Sigmoid)
+
+        def mx_th(j, i, h):
+            bank = acc.tile([P, BANK], F32, name="mx", tag="acc")
+            mx_pass(bank[:], "th", j, i, h)
+            nc.vector.tensor_tensor(out=pre[i][:, 2, :], in0=bank[:], in1=pre[i][:, 2, :], op=ALU.add)
+            if i == 0:
+                g["th"] = gates.tile([P, 2, BANK], F32, name="g_th")
+            nc.scalar.activation(out=g["th"][:, i, :], in_=pre[i][:, 2, :], func=ACT.Tanh)
+
+        def products(engine, j, h, fi, th, tiles):
             cols = slice(h * BANK, (h + 1) * BANK)
-            f, n, t = (g[gate, h][:, tiles, :] for gate in GATES)
-            engine.tensor_tensor(out=f, in0=f, in1=a_sb[j][:, tiles, cols], op=ALU.mult)
-            engine.tensor_tensor(out=t, in0=t, in1=n, op=ALU.mult)
-            engine.tensor_tensor(out=f, in0=f, in1=t, op=ALU.add)
-            nc.sync.dma_start(out=out_rows[:, 2 * j + tiles.start : 2 * j + tiles.stop, cols], in_=f)
+            engine.tensor_tensor(
+                out=fi[:, 0, tiles, :], in0=fi[:, 0, tiles, :], in1=a_sb[j][:, tiles, cols], op=ALU.mult
+            )
+            engine.tensor_tensor(out=th[:, tiles, :], in0=th[:, tiles, :], in1=fi[:, 1, tiles, :], op=ALU.mult)
+
+        def add_and_store(engine, j, h, fi, th, tiles):
+            cols = slice(h * BANK, (h + 1) * BANK)
+            o = outs.tile([P, 2, BANK], F32, name="o")
+            engine.tensor_tensor(out=o[:, tiles, :], in0=fi[:, 0, tiles, :], in1=th[:, tiles, :], op=ALU.add)
+            nc.sync.dma_start(
+                out=out_rows[:, 2 * j + tiles.start : 2 * j + tiles.stop, cols], in_=o[:, tiles, :]
+            )
 
         turn_pt()
         build_blk(0)
@@ -379,77 +403,73 @@ def tile_edrncell_pa_kernel(
         flip_x(0)
         spread_bias(0)
         flip_m(0)
+        clock[0] += 1
         run_late()
         mask_th(0)
         for h in range(1, BLOCKS):
             build_blk(h)
 
-        def finish(j, h):
-            if j == PAIRS - 1 and h >= BLOCKS - 1:
-                tail.append((j, h))
-            else:
-                combine(nc.gpsimd, j, h, slice(0, 2))
-                for gate in GATES:
-                    g.pop((gate, h))
+        behind = []
 
-        tail = []
+        def finish(j, h):
+            if j == PAIRS - 1 and h == BLOCKS - 1:
+                while behind:
+                    add_and_store(nc.gpsimd, *behind.pop(0), slice(0, 2))
+                for i in range(2):
+                    products(nc.vector, j, h, g["fi"], g["th"], slice(i, i + 1))
+                    add_and_store(nc.vector, j, h, g["fi"], g["th"], slice(i, i + 1))
+                return
+            products(nc.gpsimd, j, h, g["fi"], g["th"], slice(0, 2))
+            while behind:
+                add_and_store(nc.gpsimd, *behind.pop(0), slice(0, 2))
+            behind.append((j, h, g["fi"], g["th"]))
 
         for j in range(PAIRS):
             flips = {}
             if j + 1 < PAIRS:
                 flips = {
-                    1: lambda: flip_x(j + 1),
                     2: lambda: flip_m(j + 1),
                     4: lambda: flip_last(j + 1),
                     5: lambda: flip_a(j + 1, 0, 0),
                     6: lambda: flip_a(j + 1, 1, 0),
                     7: lambda: flip_a(j + 1, 0, 1),
                 }
+                if j > 0:
+                    flips[1] = lambda: flip_x(j + 1)
+            if j > 0:
+                flips[0] = lambda: flip_a(j, 1, 1)
             for h in range(BLOCKS):
                 if j == 0 and h == 0:
-                    for i in range(2):
-                        for gate in ("fg", "in"):
-                            plain(gate, j, i, h)
-                            if i == 1 and gate == "fg":
-                                flip_last(0)
-                                flip_a(0, 0, 0)
-                            if i == 1 and gate == "in":
-                                run_late()
-                        for gate in ("fg", "in"):
-                            mx(gate, j, i, h)
-                        if i == 0:
-                            quantise_th(0)
+                    plain_two(0, 0, 0)
+                    mx_two(0, 0, 0)
+                    quantise_th(0)
+                    plain_two(0, 1, 0, lambda: (flip_last(0), flip_a(0, 0, 0)))
+                    clock[0] += 1
+                    run_late()
+                    mx_two(0, 1, 0)
                     flip_a(0, 1, 0)
                     mask_th(1)
                     spread_bias(1)
-                    for i in range(2):
-                        plain("th", j, i, h)
+                    plain_th(0, 0, 0)
+                    plain_th(0, 1, 0)
                     quantise_th(1)
+                    mx_th(0, 0, 0)
+                    mx_th(0, 1, 0)
                     flip_x(1)
                     flip_a(0, 0, 1)
-                    for i in range(2):
-                        mx("th", j, i, h)
                     flip_a(0, 1, 1)
                     finish(j, h)
                     continue
                 for i in range(2):
                     step = 2 * h + i
-                    plain("fg", j, i, h)
-                    if step in flips:
-                        flips[step]()
-                    if step == 0 and j > 0:
-                        flip_a(j, 1, 1)
-                    plain("in", j, i, h)
-                    plain("th", j, i, h)
-                    for gate in GATES:
-                        mx(gate, j, i, h)
-                        if gate == "in" and step not in flips:
-                            run_late()
+                    clock[0] += 1
+                    plain_two(j, i, h, flips.get(step))
+                    plain_th(j, i, h)
+                    mx_two(j, i, h)
+                    run_late()
+                    mx_th(j, i, h)
                     if i == 0 and j == 0 and h + 1 < BLOCKS:
                         mask_th(h + 1)
                         spread_bias(h + 1)
                         quantise_th(h + 1)
                 finish(j, h)
-        for j, h in tail:
-            for i in range(2):
-                combine(nc.vector, j, h, slice(i, i + 1))

@@ -389,9 +389,8 @@ def tile_edrncell_pa_kernel(
             )
             engine.tensor_tensor(out=th[:, tiles, :], in0=th[:, tiles, :], in1=fi[:, 1, tiles, :], op=ALU.mult)
 
-        def add_and_store(engine, j, h, fi, th, tiles):
+        def add_and_store(engine, j, h, fi, th, tiles, o):
             cols = slice(h * BANK, (h + 1) * BANK)
-            o = outs.tile([P, 2, BANK], F32, name="o")
             engine.tensor_tensor(out=o[:, tiles, :], in0=fi[:, 0, tiles, :], in1=th[:, tiles, :], op=ALU.add)
             nc.sync.dma_start(
                 out=out_rows[:, 2 * j + tiles.start : 2 * j + tiles.stop, cols], in_=o[:, tiles, :]
@@ -410,19 +409,20 @@ def tile_edrncell_pa_kernel(
             build_blk(h)
 
         behind = []
+        at_end = []
+
+        def catch_up():
+            while behind:
+                o = outs.tile([P, 2, BANK], F32, name="o")
+                add_and_store(nc.gpsimd, *behind.pop(0), slice(0, 2), o)
 
         def finish(j, h):
-            if j == PAIRS - 1 and h == BLOCKS - 1:
-                while behind:
-                    add_and_store(nc.gpsimd, *behind.pop(0), slice(0, 2))
-                for i in range(2):
-                    products(nc.vector, j, h, g["fi"], g["th"], slice(i, i + 1))
-                    add_and_store(nc.vector, j, h, g["fi"], g["th"], slice(i, i + 1))
-                return
-            products(nc.gpsimd, j, h, g["fi"], g["th"], slice(0, 2))
-            while behind:
-                add_and_store(nc.gpsimd, *behind.pop(0), slice(0, 2))
-            behind.append((j, h, g["fi"], g["th"]))
+            if j == PAIRS - 1 and h >= BLOCKS - 2:
+                at_end.append((j, h, g["fi"], g["th"]))
+            else:
+                products(nc.gpsimd, j, h, g["fi"], g["th"], slice(0, 2))
+                catch_up()
+                behind.append((j, h, g["fi"], g["th"]))
 
         for j in range(PAIRS):
             flips = {}
@@ -473,3 +473,8 @@ def tile_edrncell_pa_kernel(
                         spread_bias(h + 1)
                         quantise_th(h + 1)
                 finish(j, h)
+        catch_up()
+        for j, h, fi, th in at_end:
+            for i in range(2):
+                products(nc.vector, j, h, fi, th, slice(i, i + 1))
+                add_and_store(nc.vector, j, h, fi, th, slice(i, i + 1), fi[:, 0, :, :])

@@ -234,14 +234,14 @@ def tile_edrncell_pa_kernel(
         def mask_th(h):
             raw = th_raw[h]
             own = raw[:, h, :].rearrange("p (q s) -> p q s", s=SLOTS)
-            (nc.gpsimd if h == 0 else nc.vector).tensor_tensor(
+            nc.vector.tensor_tensor(
                 out=own, in0=own, in1=not_ident[:].unsqueeze(2).to_broadcast([P, P, SLOTS]), op=ALU.mult
             )
 
         def quantise_th(h):
             raw = th_raw[h]
             grouped = stage.tile([P, BANK, 4], BF16, name="th_grouped", align_bytes=64)
-            nc.vector.tensor_copy(out=grouped[:], in_=raw[:].rearrange("p t n -> p n t"))
+            (nc.scalar.copy if h in () else nc.vector.tensor_copy)(out=grouped[:], in_=raw[:].rearrange("p t n -> p n t"))
             w = keep.tile([P, BANK], U32, name="th_words%d" % h, align_bytes=64)
             s = keep.tile([P, BANK], U8, name="th_plane%d" % h, align_bytes=64)
             nc.vector.quantize_mx(
@@ -309,9 +309,19 @@ def tile_edrncell_pa_kernel(
             for c in range(CHUNKS // 2):
                 chunk = half * (CHUNKS // 2) + c
                 nc.tensor.transpose(a_flip[:, c, :], a_sb[j][:, i, chunk * P : (chunk + 1) * P], ident_bf[:])
-            nc.scalar.activation(
-                out=aT[j, i][:, part, :], in_=a_flip[:], func=ACT.Identity, scale=not_last[:], bias=is_last[:]
-            )
+            if False:
+                nc.vector.tensor_scalar(
+                    out=aT[j, i][:, part, :],
+                    in0=a_flip[:],
+                    scalar1=not_last[:],
+                    scalar2=is_last[:],
+                    op0=ALU.mult,
+                    op1=ALU.add,
+                )
+            else:
+                nc.scalar.activation(
+                    out=aT[j, i][:, part, :], in_=a_flip[:], func=ACT.Identity, scale=not_last[:], bias=is_last[:]
+                )
 
         pre, g = {}, {}
 
@@ -342,11 +352,13 @@ def tile_edrncell_pa_kernel(
                 stop=True,
             )
 
-        def plain_two(j, i, h, between=None):
+        def plain_two(j, i, h, between=None, first=None):
             pre[i] = sums.tile([P, 3, BANK], F32, name="pre")
             for k, gate in enumerate(("fg", "in")):
                 bank = acc.tile([P, BANK], F32, name="plain", tag="acc")
                 x_passes(bank[:], gate, j, i, h)
+                if k == 0 and first is not None:
+                    first()
                 nc.vector.tensor_tensor(out=pre[i][:, k, :], in0=bank[:], in1=bias[h][:, k, :], op=ALU.add)
                 if k == 0 and between is not None:
                     between()
@@ -374,6 +386,54 @@ def tile_edrncell_pa_kernel(
                 g["fi"] = gates.tile([P, 2, 2, BANK], F32, name="g_fi")
             nc.scalar.activation(out=g["fi"][:, :, i, :], in_=pre[i][:, 0:2, :], func=ACT.Sigmoid)
 
+        def turn_units(j, i, h):
+            bank = acc.tile([P, PER_BANK, P], F32, name="turned_ps", tag="acc")
+            w, s = aq[j]
+            for c in range(PER_BANK):
+                cols = slice(c * P, (c + 1) * P)
+                nc.tensor.matmul_mx(
+                    out=bank[:, c, :],
+                    lhsT=th_words[h][:, cols].bitcast(FP8X4),
+                    lhsT_scale=th_planes[h][:, cols],
+                    rhs=w[:, i, :].bitcast(FP8X4),
+                    rhs_scale=s[:, i, :],
+                    start=True,
+                    stop=True,
+                )
+            turned[0] = stage.tile([P, PER_BANK, P], F32, name="turned")
+            nc.scalar.copy(out=turned[0][:], in_=bank[:])
+
+        turned = [None]
+
+        def whole_th(j, i, h):
+            bank = acc.tile([P, BANK], F32, name="plain", tag="acc")
+            for k in range(X_PASSES):
+                nc.tensor.matmul(
+                    bank[:], lhsT=xT[j][:, i, k, :], rhs=b_sb["th", h][:, k, :], start=(k == 0), stop=False
+                )
+                if k == 0:
+                    for c in range(PER_BANK):
+                        nc.tensor.matmul(
+                            bank[:, c * P : (c + 1) * P],
+                            lhsT=turned[0][:, c, :],
+                            rhs=ident_f32[:],
+                            is_transpose=True,
+                            start=False,
+                            stop=False,
+                        )
+            for q in range(PER_BANK):
+                chunk = h * PER_BANK + q
+                nc.tensor.matmul(
+                    bank[:, q * P : (q + 1) * P],
+                    lhsT=aT[j, i][:, chunk, :],
+                    rhs=blk[:, chunk, :, :].rearrange("q u t -> q (u t)"),
+                    start=False,
+                    stop=(q == PER_BANK - 1),
+                )
+            if i == 0:
+                g["th"] = gates.tile([P, 2, BANK], F32, name="g_th")
+            nc.scalar.activation(out=g["th"][:, i, :], in_=bank[:], func=ACT.Tanh)
+
         def mx_th(j, i, h):
             bank = acc.tile([P, BANK], F32, name="mx", tag="acc")
             mx_pass(bank[:], "th", j, i, h)
@@ -382,11 +442,13 @@ def tile_edrncell_pa_kernel(
                 g["th"] = gates.tile([P, 2, BANK], F32, name="g_th")
             nc.scalar.activation(out=g["th"][:, i, :], in_=pre[i][:, 2, :], func=ACT.Tanh)
 
-        def products(engine, j, h, fi, th, tiles):
+        def kept_part(engine, j, h, fi, tiles):
             cols = slice(h * BANK, (h + 1) * BANK)
             engine.tensor_tensor(
                 out=fi[:, 0, tiles, :], in0=fi[:, 0, tiles, :], in1=a_sb[j][:, tiles, cols], op=ALU.mult
             )
+
+        def new_part(engine, fi, th, tiles):
             engine.tensor_tensor(out=th[:, tiles, :], in0=th[:, tiles, :], in1=fi[:, 1, tiles, :], op=ALU.mult)
 
         def add_and_store(engine, j, h, fi, th, tiles, o):
@@ -396,85 +458,109 @@ def tile_edrncell_pa_kernel(
                 out=out_rows[:, 2 * j + tiles.start : 2 * j + tiles.stop, cols], in_=o[:, tiles, :]
             )
 
-        turn_pt()
-        build_blk(0)
-        turn_bias()
         flip_x(0)
-        spread_bias(0)
+        turn_bias()
+        turn_pt()
         flip_m(0)
+        for h in range(BLOCKS):
+            build_blk(h)
         clock[0] += 1
         run_late()
-        mask_th(0)
-        for h in range(1, BLOCKS):
-            build_blk(h)
 
         behind = []
-        at_end = []
+        on_vector = ((3, 2), (3, 3))
+        vector_tiles = []
 
         def catch_up():
             while behind:
                 o = outs.tile([P, 2, BANK], F32, name="o")
                 add_and_store(nc.gpsimd, *behind.pop(0), slice(0, 2), o)
 
-        def finish(j, h):
-            if j == PAIRS - 1 and h >= BLOCKS - 2:
-                at_end.append((j, h, g["fi"], g["th"]))
-            else:
-                products(nc.gpsimd, j, h, g["fi"], g["th"], slice(0, 2))
+        def vector_products():
+            while vector_tiles:
+                j, h, fi, th, i = vector_tiles.pop(0)
+                tile = slice(i, i + 1)
+                kept_part(nc.vector, j, h, fi, tile)
+                new_part(nc.vector, fi, th, tile)
+                add_and_store(nc.vector, j, h, fi, th, tile, fi[:, 0, :, :])
+
+        def early_product(j, h):
+            if (j, h) not in on_vector:
+                kept_part(nc.gpsimd, j, h, g["fi"], slice(0, 2))
+
+        def finish(j, h, i):
+            if (j, h) in on_vector:
+                vector_tiles.append((j, h, g["fi"], g["th"], i))
+            elif i == 1:
+                new_part(nc.gpsimd, g["fi"], g["th"], slice(0, 2))
                 catch_up()
                 behind.append((j, h, g["fi"], g["th"]))
 
-        for j in range(PAIRS):
-            flips = {}
-            if j + 1 < PAIRS:
-                flips = {
-                    2: lambda: flip_m(j + 1),
-                    4: lambda: flip_last(j + 1),
-                    5: lambda: flip_a(j + 1, 0, 0),
-                    6: lambda: flip_a(j + 1, 1, 0),
-                    7: lambda: flip_a(j + 1, 0, 1),
-                }
-                if j > 0:
-                    flips[1] = lambda: flip_x(j + 1)
-            if j > 0:
-                flips[0] = lambda: flip_a(j, 1, 1)
-            for h in range(BLOCKS):
-                if j == 0 and h == 0:
-                    plain_two(0, 0, 0)
-                    mx_two(0, 0, 0)
-                    quantise_th(0)
-                    plain_two(0, 1, 0, lambda: (flip_last(0), flip_a(0, 0, 0)))
-                    clock[0] += 1
-                    run_late()
-                    mx_two(0, 1, 0)
-                    flip_a(0, 1, 0)
-                    mask_th(1)
-                    spread_bias(1)
-                    plain_th(0, 0, 0)
-                    plain_th(0, 1, 0)
-                    quantise_th(1)
-                    mx_th(0, 0, 0)
-                    mx_th(0, 1, 0)
-                    flip_x(1)
-                    flip_a(0, 0, 1)
-                    flip_a(0, 1, 1)
-                    finish(j, h)
-                    continue
-                for i in range(2):
-                    step = 2 * h + i
-                    clock[0] += 1
-                    plain_two(j, i, h, flips.get(step))
-                    plain_th(j, i, h)
-                    mx_two(j, i, h)
-                    run_late()
-                    mx_th(j, i, h)
-                    if i == 0 and j == 0 and h + 1 < BLOCKS:
-                        mask_th(h + 1)
-                        spread_bias(h + 1)
-                        quantise_th(h + 1)
-                finish(j, h)
+        steps = [(j, h, i) for j in range(PAIRS) for h in range(BLOCKS) for i in range(2)]
+
+        def is_whole(j, h, i):
+            return i == 1
+
+        for n, (j, h, i) in enumerate(steps):
+            step = 2 * h + i
+            flips = {
+                0: lambda: flip_a(j, 0, 1),
+                1: lambda: flip_a(j, 1, 1),
+                2: lambda: flip_x(j + 1),
+                3: lambda: flip_m(j + 1),
+                5: lambda: flip_last(j + 1),
+                6: lambda: flip_a(j + 1, 0, 0),
+                7: lambda: flip_a(j + 1, 1, 0),
+            }
+            if j == 0:
+                flips[2] = lambda: flip_a(j, 0, 1)
+                flips[3] = lambda: (flip_a(j, 1, 1), flip_x(j + 1))
+                flips[4] = lambda: flip_m(j + 1)
+            if j + 1 == PAIRS:
+                flips = {0: flips[0], 1: flips[1]}
+            if n == 0:
+                plain_two(0, 0, 0, None, lambda: spread_bias(0))
+                mx_two(0, 0, 0)
+                mask_th(0)
+                quantise_th(0)
+                plain_two(0, 1, 0, lambda: flip_last(0))
+                clock[0] += 1
+                flip_a(0, 0, 0)
+                run_late()
+                mx_two(0, 1, 0)
+                early_product(0, 0)
+                flip_a(0, 1, 0)
+                mask_th(1)
+                plain_th(0, 0, 0)
+                plain_th(0, 1, 0)
+                spread_bias(1)
+                mx_th(0, 0, 0)
+                mx_th(0, 1, 0)
+                finish(0, 0, 1)
+                quantise_th(1)
+                continue
+            if n == 1:
+                continue
+            clock[0] += 1
+            plain_two(j, i, h, flips.get(step))
+            if is_whole(j, h, i):
+                whole_th(j, i, h)
+            else:
+                plain_th(j, i, h)
+            mx_two(j, i, h)
+            vector_products()
+            run_late()
+            if i == 1:
+                early_product(j, h)
+            if not is_whole(j, h, i):
+                mx_th(j, i, h)
+            if j == 0 and i == 0 and h + 1 < BLOCKS:
+                mask_th(h + 1)
+                spread_bias(h + 1)
+                quantise_th(h + 1)
+            finish(j, h, i)
+            if n + 1 < len(steps) and is_whole(*steps[n + 1]):
+                nj, nh, ni = steps[n + 1]
+                turn_units(nj, ni, nh)
         catch_up()
-        for j, h, fi, th in at_end:
-            for i in range(2):
-                products(nc.vector, j, h, fi, th, slice(i, i + 1))
-                add_and_store(nc.vector, j, h, fi, th, slice(i, i + 1), fi[:, 0, :, :])
+        vector_products()

@@ -98,7 +98,7 @@ def tile_edrncell_pa_kernel(
         planes = {}
         for gate in ("fg", "in"):
             planes[gate] = keep.tile([P, COLS], U8, name="plane_%s" % gate, align_bytes=64)
-            nc.vector.memset(planes[gate][:].bitcast(I32), 0)
+            nc.gpsimd.memset(planes[gate][:].bitcast(I32), 0)
         words = {}
         b_sb = {}
         th_raw = {}
@@ -156,16 +156,20 @@ def tile_edrncell_pa_kernel(
         load_a(0)
         load_b("th", 0)
         for h in range(1, BLOCKS):
-            load_th(h)
             load_b("fg", h)
             load_words("fg", h)
             load_b("in", h)
             load_words("in", h)
-            load_b("th", h)
             if h == 1:
+                load_th(1)
+                load_b("th", h)
+                load_th(2)
+                load_th(3)
+            else:
+                load_b("th", h)
+            if h == 2:
                 nc.sync.dma_start(out=x_sb[:, 2:ROW_TILES, :], in_=x_rows[:, 2:ROW_TILES, :])
                 load_m(1)
-            if h == 2:
                 load_a(1)
         for j in range(2, PAIRS):
             load_m(j)
@@ -186,8 +190,8 @@ def tile_edrncell_pa_kernel(
             out=not_last[:], in0=is_last[:], scalar1=-1.0, scalar2=1.0, op0=ALU.mult, op1=ALU.add
         )
         for s in range(SLOTS - 1):
-            nc.vector.memset(pt_in[:, :, s, 0 : s + 1], 0.0)
-        nc.vector.tensor_copy(out=pt_in[:, :, SLOTS - 1, :], in_=th_bias_in[:])
+            nc.gpsimd.memset(pt_in[:, :, s, 0 : s + 1], 0.0)
+        nc.gpsimd.tensor_copy(out=pt_in[:, :, SLOTS - 1, :], in_=th_bias_in[:])
 
         pt_rows = keep.tile([P, CHUNKS, SLOTS], BF16, name="pt_rows")
         blk = keep.tile([P, CHUNKS, UPC, SLOTS], BF16, name="blk")
@@ -230,25 +234,39 @@ def tile_edrncell_pa_kernel(
             bias[h] = both
 
         th_words, th_planes = {}, {}
+        set_pairs = (1, 1, 2)
 
         def mask_th(h):
             raw = th_raw[h]
             own = raw[:, h, :].rearrange("p (q s) -> p q s", s=SLOTS)
-            nc.vector.tensor_tensor(
+            nc.gpsimd.tensor_tensor(
                 out=own, in0=own, in1=not_ident[:].unsqueeze(2).to_broadcast([P, P, SLOTS]), op=ALU.mult
             )
 
-        def quantise_th(h):
-            raw = th_raw[h]
-            grouped = stage.tile([P, BANK, 4], BF16, name="th_grouped", align_bytes=64)
-            (nc.scalar.copy if h in () else nc.vector.tensor_copy)(out=grouped[:], in_=raw[:].rearrange("p t n -> p n t"))
-            w = keep.tile([P, BANK], U32, name="th_words%d" % h, align_bytes=64)
-            s = keep.tile([P, BANK], U8, name="th_plane%d" % h, align_bytes=64)
-            nc.vector.quantize_mx(
-                out=w[:].bitcast(FP8X4), scales=s[:], in_=grouped[:].rearrange("p n t -> p (n t)")
+        th_set = {0: (0, 0), 1: (1, 0), 2: (2, 0), 3: (2, 1)}
+        th_grouped, th_w, th_s = {}, {}, {}
+
+        def group_th(h):
+            k, place = th_set[h]
+            if place == 0:
+                n = set_pairs[k]
+                th_grouped[k] = stage.tile(
+                    [P, n, BANK, 4], BF16, name="th_grouped", tag="group%d" % n, align_bytes=64, bufs=3 - n
+                )
+                th_w[k] = keep.tile([P, n, BANK], U32, name="th_words%d" % k, align_bytes=64)
+                th_s[k] = keep.tile([P, n, BANK], U8, name="th_planes%d" % k, align_bytes=64)
+            (nc.scalar.copy if h in () else nc.vector.tensor_copy)(
+                out=th_grouped[k][:, place, :, :], in_=th_raw[h][:].rearrange("p t n -> p n t")
             )
-            th_words[h] = w
-            th_planes[h] = s
+            th_words[h] = th_w[k][:, place, :]
+            th_planes[h] = th_s[k][:, place, :]
+
+        def quantise_th(k):
+            nc.vector.quantize_mx(
+                out=th_w[k][:].rearrange("p j n -> p (j n)").bitcast(FP8X4),
+                scales=th_s[k][:].rearrange("p j n -> p (j n)"),
+                in_=th_grouped[k][:].rearrange("p j n t -> p (j n t)"),
+            )
 
         xT, mq, aq, aT = {}, {}, {}, {}
         late = []
@@ -267,15 +285,24 @@ def tile_edrncell_pa_kernel(
             xT[j] = keep.tile([P, 2, X_PASSES, P], BF16, name="xT%d" % j)
             nc.scalar.copy(out=xT[j][:], in_=x_flip[:])
 
-        def quantise_rows(name, grouped, j):
-            w = keep.tile([P, 2, P], U32, name="%s_words%d" % (name, j), align_bytes=64)
-            s = keep.tile([P, 2, P], U8, name="%s_plane%d" % (name, j), align_bytes=64)
-            nc.vector.quantize_mx(
-                out=w[:].rearrange("p i b -> p (i b)").bitcast(FP8X4),
-                scales=s[:].rearrange("p i b -> p (i b)"),
-                in_=grouped[:].rearrange("p i b t -> p (i b t)"),
+        set_of = {0: (0, 0), 1: (1, 0), 2: (2, 0), 3: (2, 1)}
+        grouped, row_words, row_planes = {}, {}, {}
+
+        def make_set(k):
+            shape = [P, set_pairs[k], 2, 2, P]
+            n = set_pairs[k]
+            grouped[k] = stage.tile(
+                shape + [4], BF16, name="grouped", tag="group%d" % n, align_bytes=64, bufs=3 - n
             )
-            return w, s
+            row_words[k] = keep.tile(shape, U32, name="row_words%d" % k, align_bytes=64)
+            row_planes[k] = keep.tile(shape, U8, name="row_planes%d" % k, align_bytes=64)
+
+        def quantise_rows(k, which):
+            nc.vector.quantize_mx(
+                out=row_words[k][:, :, which, :, :].rearrange("p j w i b -> p (j w i b)").bitcast(FP8X4),
+                scales=row_planes[k][:, :, which, :, :].rearrange("p j w i b -> p (j w i b)"),
+                in_=grouped[k][:, :, which, :, :, :].rearrange("p j w i b t -> p (j w i b t)"),
+            )
 
         def flip_m(j):
             m_flip = flip.tile([P, 2, 2, P], F32, name="m_flip", tag="flip")
@@ -283,12 +310,19 @@ def tile_edrncell_pa_kernel(
                 m_pairs = m_sb[j][:, i, :].bitcast(F32)
                 for u in range(2):
                     nc.tensor.transpose(m_flip[:, i, u, :], m_pairs[:, u : UNITS // 2 : 2], ident_f32[:])
-            grouped = stage.tile([P, 2, P, 4], BF16, name="m_grouped", align_bytes=64)
+            k, place = set_of[j]
+            if place == 0:
+                make_set(k)
             (nc.vector.tensor_copy if j == 0 else nc.scalar.copy)(
-                out=grouped[:].rearrange("p i b t -> p (i b t)").bitcast(F32).rearrange("p (i b u) -> p i b u", i=2, u=2),
+                out=grouped[k][:, place, 0, :, :, :]
+                .rearrange("p i b t -> p (i b t)")
+                .bitcast(F32)
+                .rearrange("p (i b u) -> p i b u", i=2, u=2),
                 in_=m_flip[:].rearrange("p i u b -> p i b u"),
             )
-            late.append((clock[0], lambda: mq.update({j: quantise_rows("mq", grouped, j)})))
+            mq[j] = (row_words[k][:, place, 0, :, :], row_planes[k][:, place, 0, :, :])
+            if j == 0:
+                late.append((clock[0], lambda: quantise_rows(k, slice(0, 1))))
 
         def flip_last(j):
             l_flip = flip.tile([P, 2, 4, P], BF16, name="l_flip", tag="flip")
@@ -297,9 +331,13 @@ def tile_edrncell_pa_kernel(
                     nc.tensor.transpose(
                         l_flip[:, i, t, :], a_sb[j][:, i, BANK * t + 3 : BANK * (t + 1) : SLOTS], ident_bf[:]
                     )
-            grouped = stage.tile([P, 2, P, 4], BF16, name="l_grouped", align_bytes=64)
-            nc.scalar.copy(out=grouped[:], in_=l_flip[:].rearrange("p i t b -> p i b t"))
-            late.append((clock[0], lambda: aq.update({j: quantise_rows("aq", grouped, j)})))
+            k, place = set_of[j]
+            nc.scalar.copy(out=grouped[k][:, place, 1, :, :, :], in_=l_flip[:].rearrange("p i t b -> p i b t"))
+            aq[j] = (row_words[k][:, place, 1, :, :], row_planes[k][:, place, 1, :, :])
+            if j == 0:
+                late.append((clock[0], lambda: quantise_rows(k, slice(1, 2))))
+            elif place == set_pairs[k] - 1:
+                late.append((clock[0], lambda: quantise_rows(k, slice(0, 2))))
 
         def flip_a(j, i, half):
             if half == 0:
@@ -338,7 +376,7 @@ def tile_edrncell_pa_kernel(
         def mx_pass(bank, gate, j, i, h):
             w, s = aq[j] if gate == "th" else mq[j]
             if gate == "th":
-                rhs, rhs_scale = th_words[h][:].bitcast(FP8X4), th_planes[h][:]
+                rhs, rhs_scale = th_words[h].bitcast(FP8X4), th_planes[h]
             else:
                 rhs = words[gate, h][:].bitcast(FP4X4)
                 rhs_scale = planes[gate][:, h * BANK : (h + 1) * BANK]
@@ -468,13 +506,13 @@ def tile_edrncell_pa_kernel(
         run_late()
 
         behind = []
-        on_vector = ((3, 2), (3, 3))
+        on_vector = ((3, 2, 1), (3, 3, 0), (3, 3, 1))
         vector_tiles = []
 
         def catch_up():
             while behind:
                 o = outs.tile([P, 2, BANK], F32, name="o")
-                add_and_store(nc.gpsimd, *behind.pop(0), slice(0, 2), o)
+                add_and_store(nc.gpsimd, *behind.pop(0), o)
 
         def vector_products():
             while vector_tiles:
@@ -484,44 +522,73 @@ def tile_edrncell_pa_kernel(
                 new_part(nc.vector, fi, th, tile)
                 add_and_store(nc.vector, j, h, fi, th, tile, fi[:, 0, :, :])
 
+        def gpsimd_tiles(j, h):
+            return slice(0, sum(1 for i in range(2) if (j, h, i) not in on_vector))
+
         def early_product(j, h):
-            if (j, h) not in on_vector:
-                kept_part(nc.gpsimd, j, h, g["fi"], slice(0, 2))
+            tiles = gpsimd_tiles(j, h)
+            if tiles.stop > 0:
+                kept_part(nc.gpsimd, j, h, g["fi"], tiles)
 
         def finish(j, h, i):
-            if (j, h) in on_vector:
+            tiles = gpsimd_tiles(j, h)
+            if (j, h, i) in on_vector:
                 vector_tiles.append((j, h, g["fi"], g["th"], i))
-            elif i == 1:
-                new_part(nc.gpsimd, g["fi"], g["th"], slice(0, 2))
+            if i == 1 and tiles.stop > 0:
+                new_part(nc.gpsimd, g["fi"], g["th"], tiles)
                 catch_up()
-                behind.append((j, h, g["fi"], g["th"]))
+                behind.append((j, h, g["fi"], g["th"], tiles))
+
+        def last_step(j, i, h):
+            tile = slice(i, i + 1)
+            pre[i] = sums.tile([P, 3, BANK], F32, name="pre")
+            plain_th(j, i, h)
+            mx_th(j, i, h)
+            vector_products()
+            fi, th = g["fi"], g["th"]
+            for k, gate in enumerate(("fg", "in")):
+                bank = acc.tile([P, BANK], F32, name="plain", tag="acc")
+                x_passes(bank[:], gate, j, i, h)
+                nc.vector.tensor_tensor(out=pre[i][:, k, :], in0=bank[:], in1=bias[h][:, k, :], op=ALU.add)
+                bank = acc.tile([P, BANK], F32, name="mx", tag="acc")
+                mx_pass(bank[:], gate, j, i, h)
+                nc.vector.tensor_tensor(out=pre[i][:, k, :], in0=bank[:], in1=pre[i][:, k, :], op=ALU.add)
+                nc.scalar.activation(out=fi[:, k, i, :], in_=pre[i][:, k, :], func=ACT.Sigmoid)
+                if gate == "fg":
+                    kept_part(nc.vector, j, h, fi, tile)
+            new_part(nc.vector, fi, th, tile)
+            add_and_store(nc.vector, j, h, fi, th, tile, fi[:, 0, :, :])
 
         steps = [(j, h, i) for j in range(PAIRS) for h in range(BLOCKS) for i in range(2)]
 
         def is_whole(j, h, i):
-            return i == 1
+            return False
 
         for n, (j, h, i) in enumerate(steps):
             step = 2 * h + i
-            flips = {
-                0: lambda: flip_a(j, 0, 1),
-                1: lambda: flip_a(j, 1, 1),
-                2: lambda: flip_x(j + 1),
-                3: lambda: flip_m(j + 1),
-                5: lambda: flip_last(j + 1),
-                6: lambda: flip_a(j + 1, 0, 0),
-                7: lambda: flip_a(j + 1, 1, 0),
-            }
+            flips = {0: lambda: flip_a(j, 0, 1), 1: lambda: flip_a(j, 1, 1)}
             if j == 0:
-                flips[2] = lambda: flip_a(j, 0, 1)
-                flips[3] = lambda: (flip_a(j, 1, 1), flip_x(j + 1))
-                flips[4] = lambda: flip_m(j + 1)
-            if j + 1 == PAIRS:
-                flips = {0: flips[0], 1: flips[1]}
+                flips = {
+                    2: lambda: flip_a(0, 0, 1),
+                    3: lambda: (flip_a(0, 1, 1), flip_x(1)),
+                    4: lambda: flip_m(1),
+                    5: lambda: flip_last(1),
+                }
+            if j == 1:
+                flips[2] = lambda: flip_m(2)
+                flips[3] = lambda: flip_m(3)
+                flips[4] = lambda: (flip_x(2), flip_last(2))
+                flips[5] = lambda: flip_last(3)
+            if j == 2:
+                flips[2] = lambda: flip_x(3)
+            if j + 1 < PAIRS:
+                flips[6] = lambda: flip_a(j + 1, 0, 0)
+                flips[7] = lambda: flip_a(j + 1, 1, 0)
             if n == 0:
+                mask_th(0)
                 plain_two(0, 0, 0, None, lambda: spread_bias(0))
                 mx_two(0, 0, 0)
-                mask_th(0)
+                group_th(0)
                 quantise_th(0)
                 plain_two(0, 1, 0, lambda: flip_last(0))
                 clock[0] += 1
@@ -530,18 +597,25 @@ def tile_edrncell_pa_kernel(
                 mx_two(0, 1, 0)
                 early_product(0, 0)
                 flip_a(0, 1, 0)
-                mask_th(1)
+                for h1 in range(1, BLOCKS):
+                    mask_th(h1)
                 plain_th(0, 0, 0)
                 plain_th(0, 1, 0)
                 spread_bias(1)
                 mx_th(0, 0, 0)
                 mx_th(0, 1, 0)
                 finish(0, 0, 1)
+                group_th(1)
                 quantise_th(1)
+                if is_whole(*steps[2]):
+                    turn_units(0, 0, 1)
                 continue
             if n == 1:
                 continue
             clock[0] += 1
+            if n + 1 == len(steps):
+                last_step(j, i, h)
+                continue
             plain_two(j, i, h, flips.get(step))
             if is_whole(j, h, i):
                 whole_th(j, i, h)
@@ -555,9 +629,11 @@ def tile_edrncell_pa_kernel(
             if not is_whole(j, h, i):
                 mx_th(j, i, h)
             if j == 0 and i == 0 and h + 1 < BLOCKS:
-                mask_th(h + 1)
                 spread_bias(h + 1)
-                quantise_th(h + 1)
+                if h == 1:
+                    group_th(2)
+                    group_th(3)
+                    quantise_th(2)
             finish(j, h, i)
             if n + 1 < len(steps) and is_whole(*steps[n + 1]):
                 nj, nh, ni = steps[n + 1]

@@ -75,16 +75,13 @@ def tile_edrncell_pa_kernel(
         nc.vector.memset(bias_rows[:].bitcast(I32), 0)
         pt_in = keep.tile([P, UPC, SLOTS, SLOTS], BF16, name="pt_in")
         nc.vector.memset(pt_in[:], 0.0)
-        th_bias_in = keep.tile([P, UPC, SLOTS], BF16, name="th_bias_in")
-        nc.vector.memset(th_bias_in[:], 0.0)
         warm = keep.tile([P, 1], F32, name="warm")
         nc.vector.memset(warm[:], 0.0)
+        for k, b in enumerate((b_fg, b_in, b_th)):
+            nc.scalar.dma_start(
+                out=bias_rows[k * CHUNKS : (k + 1) * CHUNKS, :], in_=b.rearrange("o (c n) -> (o c) n", c=CHUNKS)
+            )
         nc.scalar.dma_start(out=pt_in[0:CHUNKS, :, :, :], in_=A_pt_blk.rearrange("(c u) s t -> c u s t", c=CHUNKS))
-        nc.scalar.dma_start(out=bias_rows[0:CHUNKS, :], in_=b_fg.rearrange("o (c n) -> (o c) n", c=CHUNKS))
-        nc.scalar.dma_start(out=bias_rows[CHUNKS : 2 * CHUNKS, :], in_=b_in.rearrange("o (c n) -> (o c) n", c=CHUNKS))
-        nc.scalar.dma_start(
-            out=th_bias_in[0:CHUNKS, :, :], in_=b_th.rearrange("o (c u t) -> (o c) u t", c=CHUNKS, t=SLOTS)
-        )
         nc.scalar.activation(out=warm[:], in_=warm[:], func=ACT.Sigmoid)
 
         ident_f32 = keep.tile([P, P], F32, name="ident_f32")
@@ -146,8 +143,8 @@ def tile_edrncell_pa_kernel(
 
         x_sb = keep.tile([P, ROW_TILES, XDIM], BF16, name="x_sb")
         nc.sync.dma_start(out=x_sb[:, 0:2, :], in_=x_rows[:, 0:2, :])
-        load_b("fg", 0)
         load_m(0)
+        load_b("fg", 0)
         load_words("fg", 0)
         load_scales()
         load_b("in", 0)
@@ -183,43 +180,38 @@ def tile_edrncell_pa_kernel(
         nc.vector.tensor_reduce(
             out=unit_is[:], in_=ident_f32[:].rearrange("q (u s) -> q u s", s=SLOTS), axis=AX.X, op=ALU.add
         )
-        is_last = keep.tile([P, 1], F32, name="is_last")
-        nc.vector.tensor_reduce(out=is_last[:], in_=ident_f32[:, SLOTS - 1 : P : SLOTS], axis=AX.X, op=ALU.add)
-        not_last = keep.tile([P, 1], F32, name="not_last")
-        nc.vector.tensor_scalar(
-            out=not_last[:], in0=is_last[:], scalar1=-1.0, scalar2=1.0, op0=ALU.mult, op1=ALU.add
-        )
-        for s in range(SLOTS - 1):
+        unit_bf = keep.tile([P, UPC], BF16, name="unit_bf")
+        nc.vector.tensor_copy(out=unit_bf[:], in_=unit_is[:])
+        for s in range(SLOTS):
             nc.gpsimd.memset(pt_in[:, :, s, 0 : s + 1], 0.0)
-        nc.gpsimd.tensor_copy(out=pt_in[:, :, SLOTS - 1, :], in_=th_bias_in[:])
 
-        pt_rows = keep.tile([P, CHUNKS, SLOTS], BF16, name="pt_rows")
-        blk = keep.tile([P, CHUNKS, UPC, SLOTS], BF16, name="blk")
+        pt_rows = keep.tile([P, CHUNKS, SLOTS - 1], BF16, name="pt_rows")
+        blk = keep.tile([P, CHUNKS, UPC, SLOTS - 1], BF16, name="blk")
 
         def turn_pt():
-            pt_flip = flip.tile([P, SLOTS, P], BF16, name="pt_flip", tag="flip")
+            pt_flip = flip.tile([P, SLOTS - 1, P], BF16, name="pt_flip", tag="flip")
             pt_cols = pt_in[:].rearrange("p u s t -> p (u s t)")
-            for t in range(SLOTS):
-                nc.tensor.transpose(pt_flip[:, t, :], pt_cols[:, t : BANK : SLOTS], ident_bf[:])
+            for t in range(1, SLOTS):
+                nc.tensor.transpose(pt_flip[:, t - 1, :], pt_cols[:, t : BANK : SLOTS], ident_bf[:])
             nc.vector.tensor_copy(out=pt_rows[:], in_=pt_flip[:, :, 0:CHUNKS].rearrange("q t c -> q c t"))
 
         def build_blk(h):
-            shape = [P, PER_BANK, UPC, SLOTS]
+            shape = [P, PER_BANK, UPC, SLOTS - 1]
             part = slice(h * PER_BANK, (h + 1) * PER_BANK)
             nc.gpsimd.tensor_tensor(
                 out=blk[:, part, :, :],
                 in0=pt_rows[:, part, :].unsqueeze(2).to_broadcast(shape),
-                in1=unit_is[:].unsqueeze(1).unsqueeze(3).to_broadcast(shape),
+                in1=unit_bf[:].unsqueeze(1).unsqueeze(3).to_broadcast(shape),
                 op=ALU.mult,
             )
 
         bias = {}
-        bias_cols = keep.tile([P, 2 * CHUNKS], BF16, name="bias_cols")
+        bias_cols = keep.tile([P, 3 * CHUNKS], BF16, name="bias_cols")
 
         def turn_bias():
             bias_flip = flip.tile([P, P], BF16, name="bias_flip", tag="flip")
             nc.tensor.transpose(bias_flip[:], bias_rows[:], ident_bf[:])
-            nc.vector.tensor_copy(out=bias_cols[:], in_=bias_flip[:, 0 : 2 * CHUNKS])
+            nc.vector.tensor_copy(out=bias_cols[:], in_=bias_flip[:, 0 : 3 * CHUNKS])
 
         def spread_bias(h):
             spread = flip.tile([P, 2, PER_BANK, P], BF16, name="spread", tag="flip")
@@ -234,48 +226,31 @@ def tile_edrncell_pa_kernel(
             bias[h] = both
 
         th_words, th_planes = {}, {}
-        set_pairs = (1, 1, 2)
-
         def mask_th(h):
             raw = th_raw[h]
             own = raw[:, h, :].rearrange("p (q s) -> p q s", s=SLOTS)
-            nc.gpsimd.tensor_tensor(
+            (nc.vector if h == 0 else nc.gpsimd).tensor_tensor(
                 out=own, in0=own, in1=not_ident[:].unsqueeze(2).to_broadcast([P, P, SLOTS]), op=ALU.mult
             )
 
-        th_set = {0: (0, 0), 1: (1, 0), 2: (2, 0), 3: (2, 1)}
-        th_grouped, th_w, th_s = {}, {}, {}
+        th_grouped = {}
 
         def group_th(h):
-            k, place = th_set[h]
-            if place == 0:
-                n = set_pairs[k]
-                th_grouped[k] = stage.tile(
-                    [P, n, BANK, 4], BF16, name="th_grouped", tag="group%d" % n, align_bytes=64, bufs=3 - n
-                )
-                th_w[k] = keep.tile([P, n, BANK], U32, name="th_words%d" % k, align_bytes=64)
-                th_s[k] = keep.tile([P, n, BANK], U8, name="th_planes%d" % k, align_bytes=64)
-            (nc.scalar.copy if h in () else nc.vector.tensor_copy)(
-                out=th_grouped[k][:, place, :, :], in_=th_raw[h][:].rearrange("p t n -> p n t")
+            th_grouped[h] = stage.tile([P, BANK, 4], BF16, name="th_grouped", tag="group", align_bytes=64)
+            (nc.scalar.copy if h in (0,) else nc.vector.tensor_copy)(
+                out=th_grouped[h][:], in_=th_raw[h][:].rearrange("p t n -> p n t")
             )
-            th_words[h] = th_w[k][:, place, :]
-            th_planes[h] = th_s[k][:, place, :]
 
-        def quantise_th(k):
+        def quantise_th(h):
+            th_words[h] = keep.tile([P, BANK], U32, name="th_words%d" % h, align_bytes=64)
+            th_planes[h] = keep.tile([P, BANK], U8, name="th_planes%d" % h, align_bytes=64)
             nc.vector.quantize_mx(
-                out=th_w[k][:].rearrange("p j n -> p (j n)").bitcast(FP8X4),
-                scales=th_s[k][:].rearrange("p j n -> p (j n)"),
-                in_=th_grouped[k][:].rearrange("p j n t -> p (j n t)"),
+                out=th_words[h][:].bitcast(FP8X4),
+                scales=th_planes[h][:],
+                in_=th_grouped[h][:].rearrange("p n t -> p (n t)"),
             )
 
-        xT, mq, aq, aT = {}, {}, {}, {}
-        late = []
-
-        clock = [0]
-
-        def run_late():
-            while late and late[0][0] < clock[0]:
-                late.pop(0)[1]()
+        xT, aT = {}, {}
 
         def flip_x(j):
             x_flip = flip.tile([P, 2, X_PASSES, P], BF16, name="x_flip", tag="flip")
@@ -285,44 +260,37 @@ def tile_edrncell_pa_kernel(
             xT[j] = keep.tile([P, 2, X_PASSES, P], BF16, name="xT%d" % j)
             nc.scalar.copy(out=xT[j][:], in_=x_flip[:])
 
-        set_of = {0: (0, 0), 1: (1, 0), 2: (2, 0), 3: (2, 1)}
         grouped, row_words, row_planes = {}, {}, {}
 
-        def make_set(k):
-            shape = [P, set_pairs[k], 2, 2, P]
-            n = set_pairs[k]
-            grouped[k] = stage.tile(
-                shape + [4], BF16, name="grouped", tag="group%d" % n, align_bytes=64, bufs=3 - n
-            )
-            row_words[k] = keep.tile(shape, U32, name="row_words%d" % k, align_bytes=64)
-            row_planes[k] = keep.tile(shape, U8, name="row_planes%d" % k, align_bytes=64)
+        def make_rows(j):
+            grouped[j] = stage.tile([P, 2, 2, P, 4], BF16, name="grouped", tag="group", align_bytes=64)
+            row_words[j] = keep.tile([P, 2, 2, P], U32, name="row_words%d" % j, align_bytes=64)
+            row_planes[j] = keep.tile([P, 2, 2, P], U8, name="row_planes%d" % j, align_bytes=64)
 
-        def quantise_rows(k, which):
+        def quantise_rows(j, which):
             nc.vector.quantize_mx(
-                out=row_words[k][:, :, which, :, :].rearrange("p j w i b -> p (j w i b)").bitcast(FP8X4),
-                scales=row_planes[k][:, :, which, :, :].rearrange("p j w i b -> p (j w i b)"),
-                in_=grouped[k][:, :, which, :, :, :].rearrange("p j w i b t -> p (j w i b t)"),
+                out=row_words[j][:, which, :, :].rearrange("p w i b -> p (w i b)").bitcast(FP8X4),
+                scales=row_planes[j][:, which, :, :].rearrange("p w i b -> p (w i b)"),
+                in_=grouped[j][:, which, :, :, :].rearrange("p w i b t -> p (w i b t)"),
             )
 
         def flip_m(j):
             m_flip = flip.tile([P, 2, 2, P], F32, name="m_flip", tag="flip")
+            m_pairs = m_sb[j][:].rearrange("p i c -> p (i c)").bitcast(F32).rearrange("p (i b u) -> p i u b", i=2, u=2)
+            if j > 0:
+                m_split = stage.tile([P, 2, 2, P], F32, name="m_split", bufs=1)
+                nc.vector.tensor_copy(out=m_split[:], in_=m_pairs)
+                m_pairs = m_split[:]
             for i in range(2):
-                m_pairs = m_sb[j][:, i, :].bitcast(F32)
                 for u in range(2):
-                    nc.tensor.transpose(m_flip[:, i, u, :], m_pairs[:, u : UNITS // 2 : 2], ident_f32[:])
-            k, place = set_of[j]
-            if place == 0:
-                make_set(k)
+                    nc.tensor.transpose(m_flip[:, i, u, :], m_pairs[:, i, u, :], ident_f32[:])
             (nc.vector.tensor_copy if j == 0 else nc.scalar.copy)(
-                out=grouped[k][:, place, 0, :, :, :]
+                out=grouped[j][:, 0, :, :, :]
                 .rearrange("p i b t -> p (i b t)")
                 .bitcast(F32)
                 .rearrange("p (i b u) -> p i b u", i=2, u=2),
                 in_=m_flip[:].rearrange("p i u b -> p i b u"),
             )
-            mq[j] = (row_words[k][:, place, 0, :, :], row_planes[k][:, place, 0, :, :])
-            if j == 0:
-                late.append((clock[0], lambda: quantise_rows(k, slice(0, 1))))
 
         def flip_last(j):
             l_flip = flip.tile([P, 2, 4, P], BF16, name="l_flip", tag="flip")
@@ -331,13 +299,7 @@ def tile_edrncell_pa_kernel(
                     nc.tensor.transpose(
                         l_flip[:, i, t, :], a_sb[j][:, i, BANK * t + 3 : BANK * (t + 1) : SLOTS], ident_bf[:]
                     )
-            k, place = set_of[j]
-            nc.scalar.copy(out=grouped[k][:, place, 1, :, :, :], in_=l_flip[:].rearrange("p i t b -> p i b t"))
-            aq[j] = (row_words[k][:, place, 1, :, :], row_planes[k][:, place, 1, :, :])
-            if j == 0:
-                late.append((clock[0], lambda: quantise_rows(k, slice(1, 2))))
-            elif place == set_pairs[k] - 1:
-                late.append((clock[0], lambda: quantise_rows(k, slice(0, 2))))
+            nc.scalar.copy(out=grouped[j][:, 1, :, :, :], in_=l_flip[:].rearrange("p i t b -> p i b t"))
 
         def flip_a(j, i, half):
             if half == 0:
@@ -347,21 +309,9 @@ def tile_edrncell_pa_kernel(
             for c in range(CHUNKS // 2):
                 chunk = half * (CHUNKS // 2) + c
                 nc.tensor.transpose(a_flip[:, c, :], a_sb[j][:, i, chunk * P : (chunk + 1) * P], ident_bf[:])
-            if False:
-                nc.vector.tensor_scalar(
-                    out=aT[j, i][:, part, :],
-                    in0=a_flip[:],
-                    scalar1=not_last[:],
-                    scalar2=is_last[:],
-                    op0=ALU.mult,
-                    op1=ALU.add,
-                )
-            else:
-                nc.scalar.activation(
-                    out=aT[j, i][:, part, :], in_=a_flip[:], func=ACT.Identity, scale=not_last[:], bias=is_last[:]
-                )
+            nc.scalar.copy(out=aT[j, i][:, part, :], in_=a_flip[:])
 
-        pre, g = {}, {}
+        pre, fi_of, th_of = {}, {}, {}
 
         def x_passes(bank, gate, j, i, h):
             for k in range(X_PASSES):
@@ -370,28 +320,22 @@ def tile_edrncell_pa_kernel(
                     lhsT=xT[j][:, i, k, :],
                     rhs=b_sb[gate, h][:, k, :],
                     start=(k == 0),
-                    stop=(k == X_PASSES - 1 and gate != "th"),
+                    stop=(k == X_PASSES - 1),
                 )
 
         def mx_pass(bank, gate, j, i, h):
-            w, s = aq[j] if gate == "th" else mq[j]
-            if gate == "th":
-                rhs, rhs_scale = th_words[h].bitcast(FP8X4), th_planes[h]
-            else:
-                rhs = words[gate, h][:].bitcast(FP4X4)
-                rhs_scale = planes[gate][:, h * BANK : (h + 1) * BANK]
             nc.tensor.matmul_mx(
                 out=bank,
-                lhsT=w[:, i, :].bitcast(FP8X4),
-                lhsT_scale=s[:, i, :],
-                rhs=rhs,
-                rhs_scale=rhs_scale,
+                lhsT=row_words[j][:, 0, i, :].bitcast(FP8X4),
+                lhsT_scale=row_planes[j][:, 0, i, :],
+                rhs=words[gate, h][:].bitcast(FP4X4),
+                rhs_scale=planes[gate][:, h * BANK : (h + 1) * BANK],
                 start=True,
                 stop=True,
             )
 
         def plain_two(j, i, h, between=None, first=None):
-            pre[i] = sums.tile([P, 3, BANK], F32, name="pre")
+            pre[i] = sums.tile([P, 2, BANK], F32, name="pre")
             for k, gate in enumerate(("fg", "in")):
                 bank = acc.tile([P, BANK], F32, name="plain", tag="acc")
                 x_passes(bank[:], gate, j, i, h)
@@ -401,242 +345,219 @@ def tile_edrncell_pa_kernel(
                 if k == 0 and between is not None:
                     between()
 
-        def plain_th(j, i, h):
-            bank = acc.tile([P, BANK], F32, name="plain", tag="acc")
-            x_passes(bank[:], "th", j, i, h)
-            for q in range(PER_BANK):
-                chunk = h * PER_BANK + q
-                nc.tensor.matmul(
-                    bank[:, q * P : (q + 1) * P],
-                    lhsT=aT[j, i][:, chunk, :],
-                    rhs=blk[:, chunk, :, :].rearrange("q u t -> q (u t)"),
-                    start=False,
-                    stop=(q == PER_BANK - 1),
-                )
-            nc.scalar.copy(out=pre[i][:, 2, :], in_=bank[:])
-
         def mx_two(j, i, h):
             for k, gate in enumerate(("fg", "in")):
                 bank = acc.tile([P, BANK], F32, name="mx", tag="acc")
                 mx_pass(bank[:], gate, j, i, h)
                 nc.vector.tensor_tensor(out=pre[i][:, k, :], in0=bank[:], in1=pre[i][:, k, :], op=ALU.add)
             if i == 0:
-                g["fi"] = gates.tile([P, 2, 2, BANK], F32, name="g_fi")
-            nc.scalar.activation(out=g["fi"][:, :, i, :], in_=pre[i][:, 0:2, :], func=ACT.Sigmoid)
+                fi_of[j, h] = gates.tile([P, 2, 2, BANK], F32, name="g_fi")
+            nc.scalar.activation(out=fi_of[j, h][:, :, i, :], in_=pre[i][:], func=ACT.Sigmoid)
 
-        def turn_units(j, i, h):
-            bank = acc.tile([P, PER_BANK, P], F32, name="turned_ps", tag="acc")
-            w, s = aq[j]
-            for c in range(PER_BANK):
+        turned = {}
+
+        def turn_units(j, h, half):
+            if half == 0:
+                turned[j, h] = stage.tile([P, PER_BANK, 2, P], F32, name="turned")
+            bank = acc.tile([P, 2, 2, P], F32, name="turned_ps", tag="acc")
+            for k in range(2):
+                c = 2 * half + k
                 cols = slice(c * P, (c + 1) * P)
                 nc.tensor.matmul_mx(
-                    out=bank[:, c, :],
+                    out=bank[:, k, :, :].rearrange("p i b -> p (i b)"),
                     lhsT=th_words[h][:, cols].bitcast(FP8X4),
                     lhsT_scale=th_planes[h][:, cols],
-                    rhs=w[:, i, :].bitcast(FP8X4),
-                    rhs_scale=s[:, i, :],
+                    rhs=row_words[j][:, 1, :, :].rearrange("p i b -> p (i b)").bitcast(FP8X4),
+                    rhs_scale=row_planes[j][:, 1, :, :].rearrange("p i b -> p (i b)"),
                     start=True,
                     stop=True,
                 )
-            turned[0] = stage.tile([P, PER_BANK, P], F32, name="turned")
-            nc.scalar.copy(out=turned[0][:], in_=bank[:])
-
-        turned = [None]
+            for k in range(2):
+                c = 2 * half + k
+                col = 2 * CHUNKS + h * PER_BANK + c
+                nc.scalar.activation(
+                    out=turned[j, h][:, c, :, :],
+                    in_=bank[:, k, :, :],
+                    func=ACT.Identity,
+                    bias=bias_cols[:, col : col + 1],
+                )
 
         def whole_th(j, i, h):
             bank = acc.tile([P, BANK], F32, name="plain", tag="acc")
-            for k in range(X_PASSES):
+            x_pass = lambda k: nc.tensor.matmul(
+                bank[:],
+                lhsT=xT[j][:, i, k, :],
+                rhs=b_sb["th", h][:, k, :],
+                start=(k == 0),
+                stop=(k == X_PASSES - 1),
+            )
+            x_pass(0)
+            for c in range(PER_BANK):
                 nc.tensor.matmul(
-                    bank[:], lhsT=xT[j][:, i, k, :], rhs=b_sb["th", h][:, k, :], start=(k == 0), stop=False
+                    bank[:, c * P : (c + 1) * P],
+                    lhsT=turned[j, h][:, c, i, :],
+                    rhs=ident_f32[:],
+                    is_transpose=True,
+                    start=False,
+                    stop=False,
                 )
-                if k == 0:
-                    for c in range(PER_BANK):
-                        nc.tensor.matmul(
-                            bank[:, c * P : (c + 1) * P],
-                            lhsT=turned[0][:, c, :],
-                            rhs=ident_f32[:],
-                            is_transpose=True,
-                            start=False,
-                            stop=False,
-                        )
+            fed = bank[:].rearrange("p (q u t) -> p q u t", q=PER_BANK, t=SLOTS)
             for q in range(PER_BANK):
                 chunk = h * PER_BANK + q
                 nc.tensor.matmul(
-                    bank[:, q * P : (q + 1) * P],
+                    fed[:, q, :, 1:SLOTS],
                     lhsT=aT[j, i][:, chunk, :],
-                    rhs=blk[:, chunk, :, :].rearrange("q u t -> q (u t)"),
+                    rhs=blk[:, chunk, :, :],
                     start=False,
-                    stop=(q == PER_BANK - 1),
+                    stop=False,
                 )
+            x_pass(1)
             if i == 0:
-                g["th"] = gates.tile([P, 2, BANK], F32, name="g_th")
-            nc.scalar.activation(out=g["th"][:, i, :], in_=bank[:], func=ACT.Tanh)
+                th_of[j, h] = gates.tile([P, 2, BANK], F32, name="g_th")
+            nc.scalar.activation(out=th_of[j, h][:, i, :], in_=bank[:], func=ACT.Tanh)
 
-        def mx_th(j, i, h):
-            bank = acc.tile([P, BANK], F32, name="mx", tag="acc")
-            mx_pass(bank[:], "th", j, i, h)
-            nc.vector.tensor_tensor(out=pre[i][:, 2, :], in0=bank[:], in1=pre[i][:, 2, :], op=ALU.add)
-            if i == 0:
-                g["th"] = gates.tile([P, 2, BANK], F32, name="g_th")
-            nc.scalar.activation(out=g["th"][:, i, :], in_=pre[i][:, 2, :], func=ACT.Tanh)
-
-        def kept_part(engine, j, h, fi, tiles):
+        def kept_part(engine, j, h, tiles):
+            fi = fi_of[j, h]
             cols = slice(h * BANK, (h + 1) * BANK)
             engine.tensor_tensor(
                 out=fi[:, 0, tiles, :], in0=fi[:, 0, tiles, :], in1=a_sb[j][:, tiles, cols], op=ALU.mult
             )
 
-        def new_part(engine, fi, th, tiles):
+        def new_part(engine, j, h, tiles):
+            fi, th = fi_of[j, h], th_of[j, h]
             engine.tensor_tensor(out=th[:, tiles, :], in0=th[:, tiles, :], in1=fi[:, 1, tiles, :], op=ALU.mult)
 
-        def add_and_store(engine, j, h, fi, th, tiles, o):
+        def add_and_store(engine, j, h, tiles):
+            fi, th = fi_of[j, h], th_of[j, h]
+            if engine is nc.gpsimd:
+                o = outs.tile([P, 2, BANK], F32, name="o")
+            else:
+                o = fi[:, 0, :, :]
             cols = slice(h * BANK, (h + 1) * BANK)
             engine.tensor_tensor(out=o[:, tiles, :], in0=fi[:, 0, tiles, :], in1=th[:, tiles, :], op=ALU.add)
             nc.sync.dma_start(
                 out=out_rows[:, 2 * j + tiles.start : 2 * j + tiles.stop, cols], in_=o[:, tiles, :]
             )
 
+        both = slice(0, 2)
+        make_rows(0)
+        flip_m(0)
         flip_x(0)
         turn_bias()
         turn_pt()
-        flip_m(0)
         for h in range(BLOCKS):
             build_blk(h)
-        clock[0] += 1
-        run_late()
+        quantise_rows(0, slice(0, 1))
+        plain_two(0, 0, 0, None, lambda: spread_bias(0))
+        plain_two(0, 1, 0)
+        mask_th(0)
+        group_th(0)
+        mx_two(0, 0, 0)
+        kept_part(nc.gpsimd, 0, 0, slice(0, 1))
+        mx_two(0, 1, 0)
+        kept_part(nc.gpsimd, 0, 0, slice(1, 2))
+        flip_last(0)
+        spread_bias(1)
+        flip_a(0, 0, 0)
+        flip_a(0, 1, 0)
+        quantise_th(0)
+        quantise_rows(0, slice(1, 2))
+        for h in range(1, BLOCKS):
+            mask_th(h)
 
-        behind = []
-        on_vector = ((3, 2, 1), (3, 3, 0), (3, 3, 1))
-        vector_tiles = []
+        blocks = [(j, h) for j in range(PAIRS) for h in range(BLOCKS)]
+        last = len(blocks) - 1
+        on_vector = {13: 1, 14: 1, 15: 1}
+        waiting = []
 
-        def catch_up():
-            while behind:
-                o = outs.tile([P, 2, BANK], F32, name="o")
-                add_and_store(nc.gpsimd, *behind.pop(0), o)
+        def gpsimd_tiles(b):
+            return slice(0, 2 - on_vector.get(b, 0))
 
-        def vector_products():
-            while vector_tiles:
-                j, h, fi, th, i = vector_tiles.pop(0)
-                tile = slice(i, i + 1)
-                kept_part(nc.vector, j, h, fi, tile)
-                new_part(nc.vector, fi, th, tile)
-                add_and_store(nc.vector, j, h, fi, th, tile, fi[:, 0, :, :])
+        def vector_tiles(b):
+            tiles = slice(gpsimd_tiles(b).stop, 2)
+            if tiles.start < 2:
+                kept_part(nc.vector, *blocks[b], tiles)
+                new_part(nc.vector, *blocks[b], tiles)
+                add_and_store(nc.vector, *blocks[b], tiles)
 
-        def gpsimd_tiles(j, h):
-            return slice(0, sum(1 for i in range(2) if (j, h, i) not in on_vector))
+        def gpsimd_new(b):
+            if gpsimd_tiles(b).stop > 0:
+                new_part(nc.gpsimd, *blocks[b], gpsimd_tiles(b))
 
-        def early_product(j, h):
-            tiles = gpsimd_tiles(j, h)
-            if tiles.stop > 0:
-                kept_part(nc.gpsimd, j, h, g["fi"], tiles)
+        def gpsimd_kept(b):
+            if gpsimd_tiles(b).stop > 0:
+                kept_part(nc.gpsimd, *blocks[b], gpsimd_tiles(b))
 
-        def finish(j, h, i):
-            tiles = gpsimd_tiles(j, h)
-            if (j, h, i) in on_vector:
-                vector_tiles.append((j, h, g["fi"], g["th"], i))
-            if i == 1 and tiles.stop > 0:
-                new_part(nc.gpsimd, g["fi"], g["th"], tiles)
-                catch_up()
-                behind.append((j, h, g["fi"], g["th"], tiles))
+        def gpsimd_add(b):
+            if gpsimd_tiles(b).stop > 0:
+                add_and_store(nc.gpsimd, *blocks[b], gpsimd_tiles(b))
 
-        def last_step(j, i, h):
+        def last_step(j, h, i):
             tile = slice(i, i + 1)
-            pre[i] = sums.tile([P, 3, BANK], F32, name="pre")
-            plain_th(j, i, h)
-            mx_th(j, i, h)
-            vector_products()
-            fi, th = g["fi"], g["th"]
+            fi = fi_of[j, h]
             for k, gate in enumerate(("fg", "in")):
-                bank = acc.tile([P, BANK], F32, name="plain", tag="acc")
-                x_passes(bank[:], gate, j, i, h)
-                nc.vector.tensor_tensor(out=pre[i][:, k, :], in0=bank[:], in1=bias[h][:, k, :], op=ALU.add)
                 bank = acc.tile([P, BANK], F32, name="mx", tag="acc")
                 mx_pass(bank[:], gate, j, i, h)
                 nc.vector.tensor_tensor(out=pre[i][:, k, :], in0=bank[:], in1=pre[i][:, k, :], op=ALU.add)
                 nc.scalar.activation(out=fi[:, k, i, :], in_=pre[i][:, k, :], func=ACT.Sigmoid)
-                if gate == "fg":
-                    kept_part(nc.vector, j, h, fi, tile)
-            new_part(nc.vector, fi, th, tile)
-            add_and_store(nc.vector, j, h, fi, th, tile, fi[:, 0, :, :])
+            kept_part(nc.vector, j, h, tile)
+            new_part(nc.vector, j, h, tile)
+            add_and_store(nc.vector, j, h, tile)
 
-        steps = [(j, h, i) for j in range(PAIRS) for h in range(BLOCKS) for i in range(2)]
-
-        def is_whole(j, h, i):
-            return False
-
-        for n, (j, h, i) in enumerate(steps):
-            step = 2 * h + i
-            flips = {0: lambda: flip_a(j, 0, 1), 1: lambda: flip_a(j, 1, 1)}
-            if j == 0:
-                flips = {
-                    2: lambda: flip_a(0, 0, 1),
-                    3: lambda: (flip_a(0, 1, 1), flip_x(1)),
-                    4: lambda: flip_m(1),
-                    5: lambda: flip_last(1),
-                }
-            if j == 1:
-                flips[2] = lambda: flip_m(2)
-                flips[3] = lambda: flip_m(3)
-                flips[4] = lambda: (flip_x(2), flip_last(2))
-                flips[5] = lambda: flip_last(3)
-            if j == 2:
-                flips[2] = lambda: flip_x(3)
-            if j + 1 < PAIRS:
-                flips[6] = lambda: flip_a(j + 1, 0, 0)
-                flips[7] = lambda: flip_a(j + 1, 1, 0)
-            if n == 0:
-                mask_th(0)
-                plain_two(0, 0, 0, None, lambda: spread_bias(0))
-                mx_two(0, 0, 0)
-                group_th(0)
-                quantise_th(0)
-                plain_two(0, 1, 0, lambda: flip_last(0))
-                clock[0] += 1
-                flip_a(0, 0, 0)
-                run_late()
-                mx_two(0, 1, 0)
-                early_product(0, 0)
-                flip_a(0, 1, 0)
-                for h1 in range(1, BLOCKS):
-                    mask_th(h1)
-                plain_th(0, 0, 0)
-                plain_th(0, 1, 0)
-                spread_bias(1)
-                mx_th(0, 0, 0)
-                mx_th(0, 1, 0)
-                finish(0, 0, 1)
-                group_th(1)
-                quantise_th(1)
-                if is_whole(*steps[2]):
+        for b in range(1, len(blocks)):
+            j, h = blocks[b]
+            pj, ph = blocks[b - 1]
+            for i in range(2):
+                step = 2 * h + i
+                flip_steps = (0, 0, 3, 4, 5, 6, 7) if j == 0 else (0, 1, 4, 5, 2, 3, 4)
+                flips = {}
+                if j > 0:
+                    flips[flip_steps[0]] = lambda: flip_a(j, 0, 0)
+                    flips[flip_steps[1]] = lambda: flip_a(j, 1, 0)
+                flips[flip_steps[2]] = lambda: flip_a(j, 0, 1)
+                flips[flip_steps[3]] = lambda: flip_a(j, 1, 1)
+                if j + 1 < PAIRS:
+                    flips[flip_steps[4]] = lambda: (make_rows(j + 1), flip_last(j + 1))
+                    flips[flip_steps[5]] = lambda: (flip_m(j + 1), flip_x(j + 1))
+                plain_two(j, i, h, flips.get(step))
+                if j == 0 and i == 0:
+                    group_th(h)
+                if b == 1 and i == 0:
+                    turn_units(0, 0, 0)
                     turn_units(0, 0, 1)
-                continue
-            if n == 1:
-                continue
-            clock[0] += 1
-            if n + 1 == len(steps):
-                last_step(j, i, h)
-                continue
-            plain_two(j, i, h, flips.get(step))
-            if is_whole(j, h, i):
-                whole_th(j, i, h)
-            else:
-                plain_th(j, i, h)
-            mx_two(j, i, h)
-            vector_products()
-            run_late()
-            if i == 1:
-                early_product(j, h)
-            if not is_whole(j, h, i):
-                mx_th(j, i, h)
-            if j == 0 and i == 0 and h + 1 < BLOCKS:
-                spread_bias(h + 1)
-                if h == 1:
-                    group_th(2)
-                    group_th(3)
-                    quantise_th(2)
-            finish(j, h, i)
-            if n + 1 < len(steps) and is_whole(*steps[n + 1]):
-                nj, nh, ni = steps[n + 1]
-                turn_units(nj, ni, nh)
-        catch_up()
-        vector_products()
+                    mx_two(j, i, h)
+                    whole_th(pj, i, ph)
+                    quantise_th(h)
+                elif b == last and i == 0:
+                    whole_th(pj, 0, ph)
+                    whole_th(pj, 1, ph)
+                    gpsimd_new(b - 1)
+                    vector_tiles(b - 1)
+                    mx_two(j, i, h)
+                    gpsimd_add(b - 1)
+                    gpsimd_kept(b)
+                    whole_th(j, i, h)
+                elif b == last:
+                    whole_th(j, i, h)
+                    gpsimd_new(b)
+                    last_step(j, h, i)
+                    gpsimd_add(b)
+                else:
+                    whole_th(pj, i, ph)
+                    if j == 0 and i == 0:
+                        quantise_th(h)
+                    for half in (0, 1) if b == 1 else (i,):
+                        turn_units(j, h, half)
+                    if b + 1 == last:
+                        turn_units(j, h + 1, i)
+                    if i == 1:
+                        gpsimd_new(b - 1)
+                        vector_tiles(b - 1)
+                    mx_two(j, i, h)
+                if j + 1 < PAIRS and step == flip_steps[6]:
+                    quantise_rows(j + 1, slice(0, 2))
+                if i == 1 and b != last:
+                    gpsimd_kept(b)
+                    gpsimd_add(b - 1)
+                if j == 0 and i == 0 and h + 1 < BLOCKS:
+                    spread_bias(h + 1)

@@ -64,7 +64,6 @@ def tile_edrncell_pa_kernel(
         outs = stack.enter_context(tc.tile_pool(name="outs", bufs=3))
         acc = stack.enter_context(tc.psum_pool(name="acc", bufs=6))
         flip = stack.enter_context(tc.psum_pool(name="flip", bufs=2))
-        stack.enter_context(tc.manual_schedule(engines={mybir.EngineType.PE}))
 
         x_rows = x_t.rearrange("(p i) c -> p i c", i=ROW_TILES)
         m_rows = m_t.rearrange("(p i) c -> p i c", i=ROW_TILES)
@@ -77,11 +76,12 @@ def tile_edrncell_pa_kernel(
         nc.vector.memset(pt_in[:], 0.0)
         warm = keep.tile([P, 1], F32, name="warm")
         nc.vector.memset(warm[:], 0.0)
-        for k, b in enumerate((b_fg, b_in, b_th)):
+        th_rows = keep.tile([P, P], BF16, name="th_rows")
+        nc.vector.memset(th_rows[:].bitcast(I32), 0)
+        for k, b in enumerate((b_fg, b_in)):
             nc.scalar.dma_start(
                 out=bias_rows[k * CHUNKS : (k + 1) * CHUNKS, :], in_=b.rearrange("o (c n) -> (o c) n", c=CHUNKS)
             )
-        nc.scalar.dma_start(out=pt_in[0:CHUNKS, :, :, :], in_=A_pt_blk.rearrange("(c u) s t -> c u s t", c=CHUNKS))
         nc.scalar.activation(out=warm[:], in_=warm[:], func=ACT.Sigmoid)
 
         ident_f32 = keep.tile([P, P], F32, name="ident_f32")
@@ -117,13 +117,12 @@ def tile_edrncell_pa_kernel(
             )
             words[gate, h] = w
 
-        def load_scales():
-            for gate in ("fg", "in"):
-                for r in range(4):
-                    nc.sync.dma_start(
-                        out=planes[gate][r : P : 32, :].bitcast(I32),
-                        in_=given_scales[gate][0, r : 16 : 4, :].bitcast(I32),
-                    )
+        def load_scales(gate):
+            for r in range(4):
+                nc.sync.dma_start(
+                    out=planes[gate][r : P : 32, :].bitcast(I32),
+                    in_=given_scales[gate][0, r : 16 : 4, :].bitcast(I32),
+                )
 
         def load_th(h):
             raw = stage.tile([P, 4, BANK], BF16, name="th_raw", bufs=BLOCKS)
@@ -146,9 +145,12 @@ def tile_edrncell_pa_kernel(
         load_m(0)
         load_b("fg", 0)
         load_words("fg", 0)
-        load_scales()
+        load_scales("fg")
         load_b("in", 0)
         load_words("in", 0)
+        load_scales("in")
+        nc.sync.dma_start(out=pt_in[0:CHUNKS, :, :, :], in_=A_pt_blk.rearrange("(c u) s t -> c u s t", c=CHUNKS))
+        nc.sync.dma_start(out=th_rows[0:CHUNKS, :], in_=b_th.rearrange("o (c n) -> (o c) n", c=CHUNKS))
         load_th(0)
         load_a(0)
         load_b("th", 0)
@@ -206,12 +208,18 @@ def tile_edrncell_pa_kernel(
             )
 
         bias = {}
-        bias_cols = keep.tile([P, 3 * CHUNKS], BF16, name="bias_cols")
+        bias_cols = keep.tile([P, 2 * CHUNKS], BF16, name="bias_cols")
+        th_cols = keep.tile([P, CHUNKS], BF16, name="th_cols")
 
         def turn_bias():
             bias_flip = flip.tile([P, P], BF16, name="bias_flip", tag="flip")
             nc.tensor.transpose(bias_flip[:], bias_rows[:], ident_bf[:])
-            nc.vector.tensor_copy(out=bias_cols[:], in_=bias_flip[:, 0 : 3 * CHUNKS])
+            nc.vector.tensor_copy(out=bias_cols[:], in_=bias_flip[:, 0 : 2 * CHUNKS])
+
+        def turn_th_bias():
+            th_flip = flip.tile([P, P], BF16, name="th_flip", tag="flip")
+            nc.tensor.transpose(th_flip[:], th_rows[:], ident_bf[:])
+            nc.vector.tensor_copy(out=th_cols[:], in_=th_flip[:, 0:CHUNKS])
 
         def spread_bias(h):
             spread = flip.tile([P, 2, PER_BANK, P], BF16, name="spread", tag="flip")
@@ -229,7 +237,7 @@ def tile_edrncell_pa_kernel(
         def mask_th(h):
             raw = th_raw[h]
             own = raw[:, h, :].rearrange("p (q s) -> p q s", s=SLOTS)
-            (nc.vector if h == 0 else nc.gpsimd).tensor_tensor(
+            nc.gpsimd.tensor_tensor(
                 out=own, in0=own, in1=not_ident[:].unsqueeze(2).to_broadcast([P, P, SLOTS]), op=ALU.mult
             )
 
@@ -274,13 +282,20 @@ def tile_edrncell_pa_kernel(
                 in_=grouped[j][:, which, :, :, :].rearrange("p w i b t -> p (w i b t)"),
             )
 
+        m_split = {}
+
+        def split_m(j):
+            m_split[j] = stage.tile([P, 2, 2, P], F32, name="m_split", bufs=1)
+            nc.vector.tensor_copy(
+                out=m_split[j][:],
+                in_=m_sb[j][:].rearrange("p i c -> p (i c)").bitcast(F32).rearrange("p (i b u) -> p i u b", i=2, u=2),
+            )
+
         def flip_m(j):
             m_flip = flip.tile([P, 2, 2, P], F32, name="m_flip", tag="flip")
             m_pairs = m_sb[j][:].rearrange("p i c -> p (i c)").bitcast(F32).rearrange("p (i b u) -> p i u b", i=2, u=2)
             if j > 0:
-                m_split = stage.tile([P, 2, 2, P], F32, name="m_split", bufs=1)
-                nc.vector.tensor_copy(out=m_split[:], in_=m_pairs)
-                m_pairs = m_split[:]
+                m_pairs = m_split[j][:]
             for i in range(2):
                 for u in range(2):
                     nc.tensor.transpose(m_flip[:, i, u, :], m_pairs[:, i, u, :], ident_f32[:])
@@ -374,15 +389,15 @@ def tile_edrncell_pa_kernel(
                 )
             for k in range(2):
                 c = 2 * half + k
-                col = 2 * CHUNKS + h * PER_BANK + c
+                chunk = h * PER_BANK + c
                 nc.scalar.activation(
                     out=turned[j, h][:, c, :, :],
                     in_=bank[:, k, :, :],
                     func=ACT.Identity,
-                    bias=bias_cols[:, col : col + 1],
+                    bias=th_cols[:, chunk : chunk + 1],
                 )
 
-        def whole_th(j, i, h):
+        def whole_th(j, i, h, pieces=1):
             bank = acc.tile([P, BANK], F32, name="plain", tag="acc")
             x_pass = lambda k: nc.tensor.matmul(
                 bank[:],
@@ -414,7 +429,11 @@ def tile_edrncell_pa_kernel(
             x_pass(1)
             if i == 0:
                 th_of[j, h] = gates.tile([P, 2, BANK], F32, name="g_th")
-            nc.scalar.activation(out=th_of[j, h][:, i, :], in_=bank[:], func=ACT.Tanh)
+            width = BANK // pieces
+            for c in range(0, BANK, width):
+                nc.scalar.activation(
+                    out=th_of[j, h][:, i, c : c + width], in_=bank[:, c : c + width], func=ACT.Tanh
+                )
 
         def kept_part(engine, j, h, tiles):
             fi = fi_of[j, h]
@@ -423,52 +442,56 @@ def tile_edrncell_pa_kernel(
                 out=fi[:, 0, tiles, :], in0=fi[:, 0, tiles, :], in1=a_sb[j][:, tiles, cols], op=ALU.mult
             )
 
-        def new_part(engine, j, h, tiles):
+        def new_part(engine, j, h, tiles, part=slice(0, BANK)):
             fi, th = fi_of[j, h], th_of[j, h]
-            engine.tensor_tensor(out=th[:, tiles, :], in0=th[:, tiles, :], in1=fi[:, 1, tiles, :], op=ALU.mult)
+            engine.tensor_tensor(
+                out=th[:, tiles, part], in0=th[:, tiles, part], in1=fi[:, 1, tiles, part], op=ALU.mult
+            )
 
-        def add_and_store(engine, j, h, tiles):
+        def add_and_store(engine, j, h, tiles, part=slice(0, BANK)):
             fi, th = fi_of[j, h], th_of[j, h]
             if engine is nc.gpsimd:
                 o = outs.tile([P, 2, BANK], F32, name="o")
             else:
                 o = fi[:, 0, :, :]
-            cols = slice(h * BANK, (h + 1) * BANK)
-            engine.tensor_tensor(out=o[:, tiles, :], in0=fi[:, 0, tiles, :], in1=th[:, tiles, :], op=ALU.add)
+            cols = slice(h * BANK + part.start, h * BANK + part.stop)
+            engine.tensor_tensor(
+                out=o[:, tiles, part], in0=fi[:, 0, tiles, part], in1=th[:, tiles, part], op=ALU.add
+            )
             nc.sync.dma_start(
-                out=out_rows[:, 2 * j + tiles.start : 2 * j + tiles.stop, cols], in_=o[:, tiles, :]
+                out=out_rows[:, 2 * j + tiles.start : 2 * j + tiles.stop, cols], in_=o[:, tiles, part]
             )
 
-        both = slice(0, 2)
-        make_rows(0)
-        flip_m(0)
-        flip_x(0)
-        turn_bias()
-        turn_pt()
-        for h in range(BLOCKS):
-            build_blk(h)
-        quantise_rows(0, slice(0, 1))
-        plain_two(0, 0, 0, None, lambda: spread_bias(0))
-        plain_two(0, 1, 0)
-        mask_th(0)
-        group_th(0)
-        mx_two(0, 0, 0)
-        kept_part(nc.gpsimd, 0, 0, slice(0, 1))
-        mx_two(0, 1, 0)
-        kept_part(nc.gpsimd, 0, 0, slice(1, 2))
-        flip_last(0)
-        spread_bias(1)
-        flip_a(0, 0, 0)
-        flip_a(0, 1, 0)
-        quantise_th(0)
-        quantise_rows(0, slice(1, 2))
-        for h in range(1, BLOCKS):
-            mask_th(h)
+        def head():
+            make_rows(0)
+            flip_m(0)
+            flip_x(0)
+            turn_bias()
+            quantise_rows(0, slice(0, 1))
+            plain_two(0, 0, 0, None, lambda: spread_bias(0))
+            turn_pt()
+            turn_th_bias()
+            mask_th(0)
+            for h in range(BLOCKS):
+                build_blk(h)
+            group_th(0)
+            plain_two(0, 1, 0)
+            mx_two(0, 0, 0)
+            kept_part(nc.gpsimd, 0, 0, slice(0, 1))
+            flip_last(0)
+            spread_bias(1)
+            mx_two(0, 1, 0)
+            kept_part(nc.gpsimd, 0, 0, slice(1, 2))
+            flip_a(0, 0, 0)
+            flip_a(0, 1, 0)
+            quantise_th(0)
+            quantise_rows(0, slice(1, 2))
+            for h in range(1, BLOCKS):
+                mask_th(h)
 
         blocks = [(j, h) for j in range(PAIRS) for h in range(BLOCKS)]
         last = len(blocks) - 1
         on_vector = {13: 1, 14: 1, 15: 1}
-        waiting = []
 
         def gpsimd_tiles(b):
             return slice(0, 2 - on_vector.get(b, 0))
@@ -482,7 +505,7 @@ def tile_edrncell_pa_kernel(
 
         def gpsimd_new(b):
             if gpsimd_tiles(b).stop > 0:
-                new_part(nc.gpsimd, *blocks[b], gpsimd_tiles(b))
+                new_part(nc.vector if b in (4, 7, 10, 12) else nc.gpsimd, *blocks[b], gpsimd_tiles(b))
 
         def gpsimd_kept(b):
             if gpsimd_tiles(b).stop > 0:
@@ -492,19 +515,17 @@ def tile_edrncell_pa_kernel(
             if gpsimd_tiles(b).stop > 0:
                 add_and_store(nc.gpsimd, *blocks[b], gpsimd_tiles(b))
 
-        def last_step(j, h, i):
+        def last_tile(j, h, i):
             tile = slice(i, i + 1)
-            fi = fi_of[j, h]
-            for k, gate in enumerate(("fg", "in")):
-                bank = acc.tile([P, BANK], F32, name="mx", tag="acc")
-                mx_pass(bank[:], gate, j, i, h)
-                nc.vector.tensor_tensor(out=pre[i][:, k, :], in0=bank[:], in1=pre[i][:, k, :], op=ALU.add)
-                nc.scalar.activation(out=fi[:, k, i, :], in_=pre[i][:, k, :], func=ACT.Sigmoid)
+            mx_two(j, i, h)
             kept_part(nc.vector, j, h, tile)
-            new_part(nc.vector, j, h, tile)
-            add_and_store(nc.vector, j, h, tile)
+            whole_th(j, i, h, 2)
+            width = BANK // 2
+            for c in range(0, BANK, width):
+                new_part(nc.vector, j, h, tile, slice(c, c + width))
+                add_and_store(nc.vector, j, h, tile, slice(c, c + width))
 
-        for b in range(1, len(blocks)):
+        def block(b):
             j, h = blocks[b]
             pj, ph = blocks[b - 1]
             for i in range(2):
@@ -517,7 +538,7 @@ def tile_edrncell_pa_kernel(
                 flips[flip_steps[2]] = lambda: flip_a(j, 0, 1)
                 flips[flip_steps[3]] = lambda: flip_a(j, 1, 1)
                 if j + 1 < PAIRS:
-                    flips[flip_steps[4]] = lambda: (make_rows(j + 1), flip_last(j + 1))
+                    flips[flip_steps[4]] = lambda: (make_rows(j + 1), flip_last(j + 1), split_m(j + 1))
                     flips[flip_steps[5]] = lambda: (flip_m(j + 1), flip_x(j + 1))
                 plain_two(j, i, h, flips.get(step))
                 if j == 0 and i == 0:
@@ -538,15 +559,14 @@ def tile_edrncell_pa_kernel(
                     gpsimd_kept(b)
                     whole_th(j, i, h)
                 elif b == last:
-                    whole_th(j, i, h)
                     gpsimd_new(b)
-                    last_step(j, h, i)
                     gpsimd_add(b)
+                    last_tile(j, h, i)
                 else:
                     whole_th(pj, i, ph)
                     if j == 0 and i == 0:
                         quantise_th(h)
-                    for half in (0, 1) if b == 1 else (i,):
+                    for half in (() if i == 0 else (0, 1)) if j == 0 else (i,):
                         turn_units(j, h, half)
                     if b + 1 == last:
                         turn_units(j, h + 1, i)
@@ -561,3 +581,12 @@ def tile_edrncell_pa_kernel(
                     gpsimd_add(b - 1)
                 if j == 0 and i == 0 and h + 1 < BLOCKS:
                     spread_bias(h + 1)
+
+        pinned = mybir.EngineType
+        with tc.manual_schedule(engines={pinned.PE, pinned.DVE, pinned.Activation}):
+            head()
+            for b in range(1, 2):
+                block(b)
+        with tc.manual_schedule(engines={pinned.PE}):
+            for b in range(2, len(blocks)):
+                block(b)

from contextlib import ExitStack

import concourse.bass as bass
import concourse.mybir as mybir
import concourse.tile as tile
from concourse.masks import make_identity

F32 = mybir.dt.float32
BF16 = mybir.dt.bfloat16
U8 = mybir.dt.uint8
U32 = mybir.dt.uint32
I32 = mybir.dt.int32
FP8X4 = mybir.dt.float8_e4m3fn_x4
FP4X4 = mybir.dt.float4_e2m1fn_x4
ACT = mybir.ActivationFunctionType
ALU = mybir.AluOpType
AX = mybir.AxisListType

P = 128
ROWS = 1024
ROW_TILES = ROWS // P
UNITS = 512
SLOTS = 4
COLS = UNITS * SLOTS
BANK = 512
BLOCKS = COLS // BANK
XDIM = 256
X_PASSES = XDIM // P
CHUNKS = COLS // P
PER_BANK = BANK // P
UPC = P // SLOTS
PAIRS = ROW_TILES // 2

FLOPS = 2 * ROWS * COLS * (3 * UNITS + 3 * XDIM)

GATES = ("fg", "in", "th")


def tile_edrncell_pa_kernel(
    tc,
    x_t,
    m_t,
    a_t,
    A_fg_words,
    A_fg_scales,
    A_in_words,
    A_in_scales,
    A_th,
    A_pt_blk,
    B_fg,
    B_in,
    B_th,
    b_fg,
    b_in,
    b_th,
    out,
):
    nc = tc.nc
    with ExitStack() as stack:
        keep = stack.enter_context(tc.tile_pool(name="keep", bufs=1))
        stage = stack.enter_context(tc.tile_pool(name="stage", bufs=2))
        sums = stack.enter_context(tc.tile_pool(name="sums", bufs=3))
        gates = stack.enter_context(tc.tile_pool(name="gates", bufs=3))
        outs = stack.enter_context(tc.tile_pool(name="outs", bufs=3))
        acc = stack.enter_context(tc.psum_pool(name="acc", bufs=6))
        flip = stack.enter_context(tc.psum_pool(name="flip", bufs=2))

        x_rows = x_t.rearrange("(p i) c -> p i c", i=ROW_TILES)
        m_rows = m_t.rearrange("(p i) c -> p i c", i=ROW_TILES)
        a_rows = a_t.rearrange("(p i) c -> p i c", i=ROW_TILES)
        out_rows = out.rearrange("(p i) c -> p i c", i=ROW_TILES)

        bias_rows = keep.tile([P, P], BF16, name="bias_rows")
        nc.vector.memset(bias_rows[:].bitcast(I32), 0)
        pt_in = keep.tile([P, UPC, SLOTS, SLOTS], BF16, name="pt_in")
        nc.vector.memset(pt_in[:], 0.0)
        warm = keep.tile([P, 1], F32, name="warm")
        nc.vector.memset(warm[:], 0.0)
        th_rows = keep.tile([P, P], BF16, name="th_rows")
        nc.vector.memset(th_rows[:].bitcast(I32), 0)
        for k, b in enumerate((b_fg, b_in)):
            nc.scalar.dma_start(
                out=bias_rows[k * CHUNKS : (k + 1) * CHUNKS, :], in_=b.rearrange("o (c n) -> (o c) n", c=CHUNKS)
            )
        nc.scalar.activation(out=warm[:], in_=warm[:], func=ACT.Sigmoid)

        ident_f32 = keep.tile([P, P], F32, name="ident_f32")
        make_identity(nc, ident_f32[:])
        ident_bf = keep.tile([P, P], BF16, name="ident_bf")
        nc.vector.tensor_copy(out=ident_bf[:], in_=ident_f32[:])

        given_words = {"fg": A_fg_words, "in": A_in_words}
        given_scales = {"fg": A_fg_scales, "in": A_in_scales}
        b_dram = {"fg": B_fg, "in": B_in, "th": B_th}
        planes = {}
        for gate in ("fg", "in"):
            planes[gate] = keep.tile([P, COLS], U8, name="plane_%s" % gate, align_bytes=64)
            nc.gpsimd.memset(planes[gate][:].bitcast(I32), 0)
        words = {}
        b_sb = {}
        th_raw = {}
        m_sb = {}
        a_sb = {}

        def load_b(gate, h):
            t = keep.tile([P, X_PASSES, BANK], BF16, name="b_%s%d" % (gate, h))
            nc.sync.dma_start(
                out=t[:], in_=b_dram[gate].rearrange("(k p) n -> p k n", p=P)[:, :, h * BANK : (h + 1) * BANK]
            )
            b_sb[gate, h] = t

        def load_words(gate, h):
            w = keep.tile([P, 2 * BANK], U8, name="words_%s%d" % (gate, h), align_bytes=64)
            nc.sync.dma_start(
                out=w[:].bitcast(I32),
                in_=given_words[gate][0, :, 2 * h * BANK : 2 * (h + 1) * BANK].bitcast(I32),
            )
            words[gate, h] = w

        def load_scales(gate):
            for r in range(4):
                nc.sync.dma_start(
                    out=planes[gate][r : P : 32, :].bitcast(I32),
                    in_=given_scales[gate][0, r : 16 : 4, :].bitcast(I32),
                )

        def load_th(h):
            raw = stage.tile([P, 4, BANK], BF16, name="th_raw", bufs=BLOCKS)
            nc.sync.dma_start(
                out=raw[:], in_=A_th.rearrange("(t p) n -> p t n", p=P)[:, :, h * BANK : (h + 1) * BANK]
            )
            th_raw[h] = raw

        def load_m(j):
            m_sb[j] = keep.tile([P, 2, UNITS], BF16, name="m_sb%d" % j)
            nc.sync.dma_start(out=m_sb[j][:], in_=m_rows[:, 2 * j : 2 * j + 2, :])

        def load_a(j):
            a_sb[j] = keep.tile([P, 2, COLS], BF16, name="a_sb%d" % j)
            for i in range(2):
                nc.sync.dma_start(out=a_sb[j][:, i, :], in_=a_rows[:, 2 * j + i, :])

        x_sb = keep.tile([P, ROW_TILES, XDIM], BF16, name="x_sb")
        nc.sync.dma_start(out=x_sb[:, 0:2, :], in_=x_rows[:, 0:2, :])
        load_m(0)
        load_b("fg", 0)
        load_words("fg", 0)
        load_scales("fg")
        load_b("in", 0)
        load_words("in", 0)
        load_scales("in")
        nc.sync.dma_start(out=pt_in[0:CHUNKS, :, :, :], in_=A_pt_blk.rearrange("(c u) s t -> c u s t", c=CHUNKS))
        nc.sync.dma_start(out=th_rows[0:CHUNKS, :], in_=b_th.rearrange("o (c n) -> (o c) n", c=CHUNKS))
        load_th(0)
        load_a(0)
        load_b("th", 0)
        for h in range(1, BLOCKS):
            load_b("fg", h)
            load_words("fg", h)
            load_b("in", h)
            load_words("in", h)
            if h == 1:
                load_th(1)
                load_b("th", h)
                load_th(2)
                load_th(3)
            else:
                load_b("th", h)
            if h == 2:
                nc.sync.dma_start(out=x_sb[:, 2:ROW_TILES, :], in_=x_rows[:, 2:ROW_TILES, :])
                load_m(1)
                load_a(1)
        for j in range(2, PAIRS):
            load_m(j)
            load_a(j)

        not_ident = keep.tile([P, P], BF16, name="not_ident")
        nc.vector.tensor_scalar(
            out=not_ident[:], in0=ident_bf[:], scalar1=-1.0, scalar2=1.0, op0=ALU.mult, op1=ALU.add
        )
        unit_is = keep.tile([P, UPC], F32, name="unit_is")
        nc.vector.tensor_reduce(
            out=unit_is[:], in_=ident_f32[:].rearrange("q (u s) -> q u s", s=SLOTS), axis=AX.X, op=ALU.add
        )
        unit_bf = keep.tile([P, UPC], BF16, name="unit_bf")
        nc.vector.tensor_copy(out=unit_bf[:], in_=unit_is[:])
        for s in range(SLOTS):
            nc.gpsimd.memset(pt_in[:, :, s, 0 : s + 1], 0.0)

        pt_rows = keep.tile([P, CHUNKS, SLOTS - 1], BF16, name="pt_rows")
        blk = keep.tile([P, CHUNKS, UPC, SLOTS - 1], BF16, name="blk")

        def turn_pt():
            pt_flip = flip.tile([P, SLOTS - 1, P], BF16, name="pt_flip", tag="flip")
            pt_cols = pt_in[:].rearrange("p u s t -> p (u s t)")
            for t in range(1, SLOTS):
                nc.tensor.transpose(pt_flip[:, t - 1, :], pt_cols[:, t : BANK : SLOTS], ident_bf[:])
            nc.vector.tensor_copy(out=pt_rows[:], in_=pt_flip[:, :, 0:CHUNKS].rearrange("q t c -> q c t"))

        def build_blk(h):
            shape = [P, PER_BANK, UPC, SLOTS - 1]
            part = slice(h * PER_BANK, (h + 1) * PER_BANK)
            nc.gpsimd.tensor_tensor(
                out=blk[:, part, :, :],
                in0=pt_rows[:, part, :].unsqueeze(2).to_broadcast(shape),
                in1=unit_bf[:].unsqueeze(1).unsqueeze(3).to_broadcast(shape),
                op=ALU.mult,
            )

        bias = {}
        bias_cols = keep.tile([P, 2 * CHUNKS], BF16, name="bias_cols")
        th_cols = keep.tile([P, CHUNKS], BF16, name="th_cols")

        def turn_bias():
            bias_flip = flip.tile([P, P], BF16, name="bias_flip", tag="flip")
            nc.tensor.transpose(bias_flip[:], bias_rows[:], ident_bf[:])
            nc.vector.tensor_copy(out=bias_cols[:], in_=bias_flip[:, 0 : 2 * CHUNKS])

        def turn_th_bias():
            th_flip = flip.tile([P, P], BF16, name="th_flip", tag="flip")
            nc.tensor.transpose(th_flip[:], th_rows[:], ident_bf[:])
            nc.vector.tensor_copy(out=th_cols[:], in_=th_flip[:, 0:CHUNKS])

        def spread_bias(h):
            spread = flip.tile([P, 2, PER_BANK, P], BF16, name="spread", tag="flip")
            both = keep.tile([P, 2, BANK], BF16, name="bias%d" % h)
            for k in range(2):
                for q in range(PER_BANK):
                    col = k * CHUNKS + h * PER_BANK + q
                    nc.tensor.transpose(
                        spread[:, k, q, :], bias_cols[:, col : col + 1].to_broadcast([P, P]), ident_bf[:]
                    )
            nc.scalar.copy(out=both[:], in_=spread[:].rearrange("p k q n -> p k (q n)"))
            bias[h] = both

        th_words, th_planes = {}, {}
        def mask_th(h):
            raw = th_raw[h]
            own = raw[:, h, :].rearrange("p (q s) -> p q s", s=SLOTS)
            nc.gpsimd.tensor_tensor(
                out=own, in0=own, in1=not_ident[:].unsqueeze(2).to_broadcast([P, P, SLOTS]), op=ALU.mult
            )

        th_grouped = {}

        def group_th(h):
            th_grouped[h] = stage.tile([P, BANK, 4], BF16, name="th_grouped", tag="group", align_bytes=64)
            (nc.scalar.copy if h in (0,) else nc.vector.tensor_copy)(
                out=th_grouped[h][:], in_=th_raw[h][:].rearrange("p t n -> p n t")
            )

        def quantise_th(h):
            th_words[h] = keep.tile([P, BANK], U32, name="th_words%d" % h, align_bytes=64)
            th_planes[h] = keep.tile([P, BANK], U8, name="th_planes%d" % h, align_bytes=64)
            nc.vector.quantize_mx(
                out=th_words[h][:].bitcast(FP8X4),
                scales=th_planes[h][:],
                in_=th_grouped[h][:].rearrange("p n t -> p (n t)"),
            )

        xT, aT = {}, {}

        def flip_x(j):
            x_flip = flip.tile([P, 2, X_PASSES, P], BF16, name="x_flip", tag="flip")
            for i in range(2):
                for k in range(X_PASSES):
                    nc.tensor.transpose(x_flip[:, i, k, :], x_sb[:, 2 * j + i, k * P : (k + 1) * P], ident_bf[:])
            xT[j] = keep.tile([P, 2, X_PASSES, P], BF16, name="xT%d" % j)
            nc.scalar.copy(out=xT[j][:], in_=x_flip[:])

        grouped, row_words, row_planes = {}, {}, {}

        def make_rows(j):
            grouped[j] = stage.tile([P, 2, 2, P, 4], BF16, name="grouped", tag="group", align_bytes=64)
            row_words[j] = keep.tile([P, 2, 2, P], U32, name="row_words%d" % j, align_bytes=64)
            row_planes[j] = keep.tile([P, 2, 2, P], U8, name="row_planes%d" % j, align_bytes=64)

        def quantise_rows(j, which):
            nc.vector.quantize_mx(
                out=row_words[j][:, which, :, :].rearrange("p w i b -> p (w i b)").bitcast(FP8X4),
                scales=row_planes[j][:, which, :, :].rearrange("p w i b -> p (w i b)"),
                in_=grouped[j][:, which, :, :, :].rearrange("p w i b t -> p (w i b t)"),
            )

        m_split = {}

        def split_m(j):
            m_split[j] = stage.tile([P, 2, 2, P], F32, name="m_split", bufs=1)
            nc.vector.tensor_copy(
                out=m_split[j][:],
                in_=m_sb[j][:].rearrange("p i c -> p (i c)").bitcast(F32).rearrange("p (i b u) -> p i u b", i=2, u=2),
            )

        def flip_m(j):
            m_flip = flip.tile([P, 2, 2, P], F32, name="m_flip", tag="flip")
            m_pairs = m_sb[j][:].rearrange("p i c -> p (i c)").bitcast(F32).rearrange("p (i b u) -> p i u b", i=2, u=2)
            if j > 0:
                m_pairs = m_split[j][:]
            for i in range(2):
                for u in range(2):
                    nc.tensor.transpose(m_flip[:, i, u, :], m_pairs[:, i, u, :], ident_f32[:])
            (nc.vector.tensor_copy if j == 0 else nc.scalar.copy)(
                out=grouped[j][:, 0, :, :, :]
                .rearrange("p i b t -> p (i b t)")
                .bitcast(F32)
                .rearrange("p (i b u) -> p i b u", i=2, u=2),
                in_=m_flip[:].rearrange("p i u b -> p i b u"),
            )

        def flip_last(j):
            l_flip = flip.tile([P, 2, 4, P], BF16, name="l_flip", tag="flip")
            for i in range(2):
                for t in range(4):
                    nc.tensor.transpose(
                        l_flip[:, i, t, :], a_sb[j][:, i, BANK * t + 3 : BANK * (t + 1) : SLOTS], ident_bf[:]
                    )
            nc.scalar.copy(out=grouped[j][:, 1, :, :, :], in_=l_flip[:].rearrange("p i t b -> p i b t"))

        def flip_a(j, i, half):
            if half == 0:
                aT[j, i] = stage.tile([P, CHUNKS, P], BF16, name="aT", bufs=4)
            part = slice(half * (CHUNKS // 2), (half + 1) * (CHUNKS // 2))
            a_flip = flip.tile([P, CHUNKS // 2, P], BF16, name="a_flip", tag="flip")
            for c in range(CHUNKS // 2):
                chunk = half * (CHUNKS // 2) + c
                nc.tensor.transpose(a_flip[:, c, :], a_sb[j][:, i, chunk * P : (chunk + 1) * P], ident_bf[:])
            nc.scalar.copy(out=aT[j, i][:, part, :], in_=a_flip[:])

        pre, fi_of, th_of = {}, {}, {}

        def x_passes(bank, gate, j, i, h):
            for k in range(X_PASSES):
                nc.tensor.matmul(
                    bank,
                    lhsT=xT[j][:, i, k, :],
                    rhs=b_sb[gate, h][:, k, :],
                    start=(k == 0),
                    stop=(k == X_PASSES - 1),
                )

        def mx_pass(bank, gate, j, i, h):
            nc.tensor.matmul_mx(
                out=bank,
                lhsT=row_words[j][:, 0, i, :].bitcast(FP8X4),
                lhsT_scale=row_planes[j][:, 0, i, :],
                rhs=words[gate, h][:].bitcast(FP4X4),
                rhs_scale=planes[gate][:, h * BANK : (h + 1) * BANK],
                start=True,
                stop=True,
            )

        def plain_two(j, i, h, between=None, first=None):
            pre[i] = sums.tile([P, 2, BANK], F32, name="pre")
            for k, gate in enumerate(("fg", "in")):
                bank = acc.tile([P, BANK], F32, name="plain", tag="acc")
                x_passes(bank[:], gate, j, i, h)
                if k == 0 and first is not None:
                    first()
                nc.vector.tensor_tensor(out=pre[i][:, k, :], in0=bank[:], in1=bias[h][:, k, :], op=ALU.add)
                if k == 0 and between is not None:
                    between()

        def mx_two(j, i, h):
            for k, gate in enumerate(("fg", "in")):
                bank = acc.tile([P, BANK], F32, name="mx", tag="acc")
                mx_pass(bank[:], gate, j, i, h)
                nc.vector.tensor_tensor(out=pre[i][:, k, :], in0=bank[:], in1=pre[i][:, k, :], op=ALU.add)
            if i == 0:
                fi_of[j, h] = gates.tile([P, 2, 2, BANK], F32, name="g_fi")
            nc.scalar.activation(out=fi_of[j, h][:, :, i, :], in_=pre[i][:], func=ACT.Sigmoid)

        turned = {}

        def turn_units(j, h, half):
            if half == 0:
                turned[j, h] = stage.tile([P, PER_BANK, 2, P], F32, name="turned")
            bank = acc.tile([P, 2, 2, P], F32, name="turned_ps", tag="acc")
            for k in range(2):
                c = 2 * half + k
                cols = slice(c * P, (c + 1) * P)
                nc.tensor.matmul_mx(
                    out=bank[:, k, :, :].rearrange("p i b -> p (i b)"),
                    lhsT=th_words[h][:, cols].bitcast(FP8X4),
                    lhsT_scale=th_planes[h][:, cols],
                    rhs=row_words[j][:, 1, :, :].rearrange("p i b -> p (i b)").bitcast(FP8X4),
                    rhs_scale=row_planes[j][:, 1, :, :].rearrange("p i b -> p (i b)"),
                    start=True,
                    stop=True,
                )
            for k in range(2):
                c = 2 * half + k
                chunk = h * PER_BANK + c
                nc.scalar.activation(
                    out=turned[j, h][:, c, :, :],
                    in_=bank[:, k, :, :],
                    func=ACT.Identity,
                    bias=th_cols[:, chunk : chunk + 1],
                )

        def whole_th(j, i, h, pieces=1):
            bank = acc.tile([P, BANK], F32, name="plain", tag="acc")
            x_pass = lambda k: nc.tensor.matmul(
                bank[:],
                lhsT=xT[j][:, i, k, :],
                rhs=b_sb["th", h][:, k, :],
                start=(k == 0),
                stop=(k == X_PASSES - 1),
            )
            x_pass(0)
            for c in range(PER_BANK):
                nc.tensor.matmul(
                    bank[:, c * P : (c + 1) * P],
                    lhsT=turned[j, h][:, c, i, :],
                    rhs=ident_f32[:],
                    is_transpose=True,
                    start=False,
                    stop=False,
                )
            fed = bank[:].rearrange("p (q u t) -> p q u t", q=PER_BANK, t=SLOTS)
            for q in range(PER_BANK):
                chunk = h * PER_BANK + q
                nc.tensor.matmul(
                    fed[:, q, :, 1:SLOTS],
                    lhsT=aT[j, i][:, chunk, :],
                    rhs=blk[:, chunk, :, :],
                    start=False,
                    stop=False,
                )
            x_pass(1)
            if i == 0:
                th_of[j, h] = gates.tile([P, 2, BANK], F32, name="g_th")
            width = BANK // pieces
            for c in range(0, BANK, width):
                nc.scalar.activation(
                    out=th_of[j, h][:, i, c : c + width], in_=bank[:, c : c + width], func=ACT.Tanh
                )

        def kept_part(engine, j, h, tiles):
            fi = fi_of[j, h]
            cols = slice(h * BANK, (h + 1) * BANK)
            engine.tensor_tensor(
                out=fi[:, 0, tiles, :], in0=fi[:, 0, tiles, :], in1=a_sb[j][:, tiles, cols], op=ALU.mult
            )

        def new_part(engine, j, h, tiles, part=slice(0, BANK)):
            fi, th = fi_of[j, h], th_of[j, h]
            engine.tensor_tensor(
                out=th[:, tiles, part], in0=th[:, tiles, part], in1=fi[:, 1, tiles, part], op=ALU.mult
            )

        def add_and_store(engine, j, h, tiles, part=slice(0, BANK)):
            fi, th = fi_of[j, h], th_of[j, h]
            if engine is nc.gpsimd:
                o = outs.tile([P, 2, BANK], F32, name="o")
            else:
                o = fi[:, 0, :, :]
            cols = slice(h * BANK + part.start, h * BANK + part.stop)
            engine.tensor_tensor(
                out=o[:, tiles, part], in0=fi[:, 0, tiles, part], in1=th[:, tiles, part], op=ALU.add
            )
            nc.sync.dma_start(
                out=out_rows[:, 2 * j + tiles.start : 2 * j + tiles.stop, cols], in_=o[:, tiles, part]
            )

        def head():
            make_rows(0)
            flip_m(0)
            flip_x(0)
            turn_bias()
            quantise_rows(0, slice(0, 1))
            plain_two(0, 0, 0, None, lambda: spread_bias(0))
            turn_pt()
            turn_th_bias()
            mask_th(0)
            for h in range(BLOCKS):
                build_blk(h)
            group_th(0)
            plain_two(0, 1, 0)
            mx_two(0, 0, 0)
            kept_part(nc.gpsimd, 0, 0, slice(0, 1))
            flip_last(0)
            spread_bias(1)
            mx_two(0, 1, 0)
            kept_part(nc.gpsimd, 0, 0, slice(1, 2))
            flip_a(0, 0, 0)
            flip_a(0, 1, 0)
            quantise_th(0)
            quantise_rows(0, slice(1, 2))
            for h in range(1, BLOCKS):
                mask_th(h)

        blocks = [(j, h) for j in range(PAIRS) for h in range(BLOCKS)]
        last = len(blocks) - 1
        on_vector = {13: 1, 14: 1, 15: 1}

        def gpsimd_tiles(b):
            return slice(0, 2 - on_vector.get(b, 0))

        def vector_tiles(b):
            tiles = slice(gpsimd_tiles(b).stop, 2)
            if tiles.start < 2:
                kept_part(nc.vector, *blocks[b], tiles)
                new_part(nc.vector, *blocks[b], tiles)
                add_and_store(nc.vector, *blocks[b], tiles)

        def gpsimd_new(b):
            if gpsimd_tiles(b).stop > 0:
                new_part(nc.vector if b in (4, 7, 10, 12) else nc.gpsimd, *blocks[b], gpsimd_tiles(b))

        def gpsimd_kept(b):
            if gpsimd_tiles(b).stop > 0:
                kept_part(nc.gpsimd, *blocks[b], gpsimd_tiles(b))

        def gpsimd_add(b):
            if gpsimd_tiles(b).stop > 0:
                add_and_store(nc.gpsimd, *blocks[b], gpsimd_tiles(b))

        def last_tile(j, h, i):
            tile = slice(i, i + 1)
            mx_two(j, i, h)
            kept_part(nc.vector, j, h, tile)
            whole_th(j, i, h, 2)
            width = BANK // 2
            for c in range(0, BANK, width):
                new_part(nc.vector, j, h, tile, slice(c, c + width))
                add_and_store(nc.vector, j, h, tile, slice(c, c + width))

        def block(b):
            j, h = blocks[b]
            pj, ph = blocks[b - 1]
            for i in range(2):
                step = 2 * h + i
                flip_steps = (0, 0, 3, 4, 5, 6, 7) if j == 0 else (0, 1, 4, 5, 2, 3, 4)
                flips = {}
                if j > 0:
                    flips[flip_steps[0]] = lambda: flip_a(j, 0, 0)
                    flips[flip_steps[1]] = lambda: flip_a(j, 1, 0)
                flips[flip_steps[2]] = lambda: flip_a(j, 0, 1)
                flips[flip_steps[3]] = lambda: flip_a(j, 1, 1)
                if j + 1 < PAIRS:
                    flips[flip_steps[4]] = lambda: (make_rows(j + 1), flip_last(j + 1), split_m(j + 1))
                    flips[flip_steps[5]] = lambda: (flip_m(j + 1), flip_x(j + 1))
                plain_two(j, i, h, flips.get(step))
                if j == 0 and i == 0:
                    group_th(h)
                if b == 1 and i == 0:
                    turn_units(0, 0, 0)
                    turn_units(0, 0, 1)
                    mx_two(j, i, h)
                    whole_th(pj, i, ph)
                    quantise_th(h)
                elif b == last and i == 0:
                    whole_th(pj, 0, ph)
                    whole_th(pj, 1, ph)
                    gpsimd_new(b - 1)
                    vector_tiles(b - 1)
                    mx_two(j, i, h)
                    gpsimd_add(b - 1)
                    gpsimd_kept(b)
                    whole_th(j, i, h)
                elif b == last:
                    gpsimd_new(b)
                    gpsimd_add(b)
                    last_tile(j, h, i)
                else:
                    whole_th(pj, i, ph)
                    if j == 0 and i == 0:
                        quantise_th(h)
                    for half in (() if i == 0 else (0, 1)) if j == 0 else (i,):
                        turn_units(j, h, half)
                    if b + 1 == last:
                        turn_units(j, h + 1, i)
                    if i == 1:
                        gpsimd_new(b - 1)
                        vector_tiles(b - 1)
                    mx_two(j, i, h)
                if j + 1 < PAIRS and step == flip_steps[6]:
                    quantise_rows(j + 1, slice(0, 2))
                if i == 1 and b != last:
                    gpsimd_kept(b)
                    gpsimd_add(b - 1)
                if j == 0 and i == 0 and h + 1 < BLOCKS:
                    spread_bias(h + 1)

        pinned = mybir.EngineType
        with tc.manual_schedule(engines={pinned.PE, pinned.DVE, pinned.Activation}):
            head()
            for b in range(1, 2):
                block(b)
        with tc.manual_schedule(engines={pinned.PE}):
            for b in range(2, len(blocks)):
                block(b)
